import numpy as np
import ml_dtypes


def mxq(x, axis, fmt="e4m3"):
    dtype, down = {"e4m3": (ml_dtypes.float8_e4m3fn, 7), "e5m2": (ml_dtypes.float8_e5m2, 14)}[fmt]
    v = np.moveaxis(np.asarray(x, np.float32).astype(ml_dtypes.bfloat16).astype(np.float64), axis, -1)
    blocks = v.reshape(v.shape[:-1] + (-1, 32))
    amax = np.abs(blocks).max(-1, keepdims=True)
    byte = np.maximum(np.where(amax > 0, np.frexp(amax)[1] - 1 + 127, 0) - down, 1)
    scale = np.exp2(byte - 127.0)
    codes = (blocks / scale).astype(np.float32).astype(dtype).astype(np.float64)
    return np.moveaxis((codes * scale).reshape(v.shape), -1, axis)


WIDE = False


def mx_kscale(k):
    if not WIDE:
        return np.ones(k)
    levels = np.array([10, -10, 5, -5, 0])
    a = np.random.permutation(np.resize(levels, k // 512 * 4)).reshape(k // 512, 4)
    idx = np.arange(k)
    return np.exp2(a[idx // 512, idx % 128 // 32])


BF16 = ml_dtypes.bfloat16


def bf(x):
    return np.asarray(x, np.float32).astype(BF16)


def f64(x):
    return np.asarray(x).astype(np.float64)


N, KS, C, ATT, MID = 16, 512, 1024, 256, 512


def setup_inputs():
    s = mx_kscale(C)
    a = 1.7 / ATT ** 0.25
    return {"x": bf(np.random.standard_normal((N, KS, C)) * s),
            "W_psi": bf(np.random.standard_normal((ATT, C)) / np.sqrt(C) / s),
            "b_psi": bf(np.random.standard_normal(ATT) * 0.3),
            "x_phi": bf(np.random.standard_normal((N, KS, ATT)) * a),
            "x_theta": bf(np.random.standard_normal((N, KS, ATT)) * a)}


def reference(x, W_psi, b_psi, x_phi, x_theta):
    x3 = (mxq(f64(x), 2, "e4m3") @ mxq(f64(W_psi), 1, "e4m3").T) + f64(b_psi)
    sc = f64(x_phi) @ f64(x_theta).transpose(0, 2, 1)
    e = np.exp(sc - sc.max(axis=1, keepdims=True))
    cov = e / e.sum(axis=1, keepdims=True)
    return mxq(cov, 2, "e4m3") @ mxq(x3, 1, "e4m3")

@@ -1,0 +1,250 @@
+from contextlib import ExitStack
+
+import concourse.mybir as mybir
+from concourse.masks import make_identity
+
+F32 = mybir.dt.float32
+BF16 = mybir.dt.bfloat16
+U32 = mybir.dt.uint32
+U8 = mybir.dt.uint8
+FP8X4 = mybir.dt.float8_e4m3fn_x4
+
+SAMPLES, TOKENS, CHANNELS, FEATURES = 16, 512, 1024, 256
+P = 128
+PACK = 4
+QUARTERS = TOKENS // P
+PASSES = CHANNELS // (P * PACK)
+HALVES = FEATURES // P
+WORDS = CHANNELS // 2
+
+FLOPS = 2 * SAMPLES * TOKENS * (CHANNELS * FEATURES + 2 * TOKENS * FEATURES)
+
+
+def tile_vc_interaction_sa_module_pa_t_kernel(tc, x, W_psi, b_psi, x_phi, x_theta, out):
+    nc = tc.nc
+    with ExitStack() as ctx:
+        consts = ctx.enter_context(tc.tile_pool(name="consts", bufs=1))
+        loads = ctx.enter_context(tc.tile_pool(name="loads", bufs=3))
+        work = ctx.enter_context(tc.tile_pool(name="work", bufs=3))
+        psum_tr = ctx.enter_context(tc.psum_pool(name="psum_tr", bufs=3))
+        psum_sc = ctx.enter_context(tc.psum_pool(name="psum_sc", bufs=2))
+        psum_mx = ctx.enter_context(tc.psum_pool(name="psum_mx", bufs=3))
+
+        x_sb, phi_sb, theta_sb = {}, {}, {}
+        x_grouped, x_codes, x_scales = {}, {}, {}
+        phi_t, theta_t = {}, {}
+        neg_max, exp_sum, inv_sum, expo = {}, {}, {}, {}
+        cov_grouped, cov_codes, cov_scales = {}, {}, {}
+        x3_bank, x3_grouped, x3_codes, x3_scales = {}, {}, {}, {}
+
+        def live(n):
+            return 0 <= n < SAMPLES
+
+        def by_quarters(rows):
+            return rows.rearrange("(p t) w -> p (t w)", t=QUARTERS)
+
+        def load_sample(n):
+            x_sb[n] = loads.tile([P, QUARTERS * CHANNELS], BF16, name="x_sb")
+            nc.sync.dma_start(out=x_sb[n][:], in_=by_quarters(x[n]))
+            phi_sb[n] = loads.tile([P, QUARTERS * FEATURES], BF16, name="phi_sb")
+            nc.sync.dma_start(out=phi_sb[n][:], in_=by_quarters(x_phi[n]))
+            theta_sb[n] = loads.tile([P, QUARTERS * FEATURES], BF16, name="theta_sb")
+            nc.sync.dma_start(out=theta_sb[n][:], in_=by_quarters(x_theta[n]))
+
+        def transpose_channel_words(words, grouped_words, copy):
+            bank = psum_tr.tile([P, PASSES * 2, P], F32, name="word_bank", tag="tr")
+            for v in range(PASSES * 2):
+                nc.tensor.transpose(bank[:, v, :], words[:, v * P : (v + 1) * P], ident_f32[:])
+            copy(out=grouped_words, in_=bank[:].rearrange("q (g u) r -> q g r u", g=PASSES))
+
+        ident_f32 = consts.tile([P, P], F32, name="ident_f32")
+        make_identity(nc, ident_f32[:])
+        ident_bf16 = consts.tile([P, P], BF16, name="ident_bf16")
+        make_identity(nc, ident_bf16[:])
+
+        w_sb = consts.tile([P, HALVES * CHANNELS], BF16, name="w_sb")
+        nc.sync.dma_start(
+            out=w_sb[:].rearrange("p (h c) -> p h c", h=HALVES),
+            in_=W_psi.rearrange("(h p) c -> p h c", p=P),
+        )
+        load_sample(0)
+        load_sample(1)
+        bias_bf16 = consts.tile([P, FEATURES], BF16, name="bias_bf16")
+        nc.scalar.dma_start(out=bias_bf16[:], in_=b_psi.partition_broadcast(P))
+        bias = consts.tile([P, FEATURES], F32, name="bias")
+        nc.vector.tensor_copy(out=bias[:], in_=bias_bf16[:])
+
+        w_grouped = consts.tile([P, PASSES * FEATURES * PACK], BF16, name="w_grouped", align_bytes=64)
+        w_grouped_words = w_grouped[:].bitcast(F32).rearrange("q (g a u) -> q g a u", g=PASSES, u=2)
+        for h in range(HALVES):
+            transpose_channel_words(
+                w_sb[:].bitcast(F32)[:, h * WORDS : (h + 1) * WORDS],
+                w_grouped_words[:, :, h * P : (h + 1) * P, :],
+                nc.vector.tensor_copy,
+            )
+        w_codes = consts.tile([P, PASSES * FEATURES], U32, name="w_codes", align_bytes=64)
+        w_scales = consts.tile([P, PASSES * FEATURES], U8, name="w_scales", align_bytes=64)
+        nc.vector.quantize_mx(out=w_codes[:].bitcast(FP8X4), scales=w_scales[:], in_=w_grouped[:])
+
+        def transpose_x(n, t):
+            if t == 0:
+                x_codes[n] = work.tile([P, QUARTERS * PASSES * P], U32, name="x_codes", align_bytes=64)
+                x_scales[n] = work.tile([P, QUARTERS * PASSES * P], U8, name="x_scales", align_bytes=64)
+            x_grouped[n, t] = work.tile([P, PASSES * P * PACK], BF16, name="x_grouped", align_bytes=64)
+            transpose_channel_words(
+                x_sb[n][:].bitcast(F32)[:, t * WORDS : (t + 1) * WORDS],
+                x_grouped[n, t][:].bitcast(F32).rearrange("q (g r u) -> q g r u", g=PASSES, u=2),
+                nc.scalar.copy,
+            )
+
+        def quantise_x(n, t):
+            cols = slice(t * PASSES * P, (t + 1) * PASSES * P)
+            nc.vector.quantize_mx(
+                out=x_codes[n][:, cols].bitcast(FP8X4), scales=x_scales[n][:, cols], in_=x_grouped[n, t][:]
+            )
+
+        def scores_and_feature_transposes(n, t):
+            m = n + 1
+            if live(n):
+                sc_bank = psum_sc.tile([P, TOKENS], F32, name="sc_bank")
+            if live(m):
+                if t == 0:
+                    phi_t[m] = work.tile([P, HALVES, TOKENS], BF16, name="phi_t")
+                    theta_t[m] = work.tile([P, HALVES, TOKENS], BF16, name="theta_t")
+                source, target = (phi_sb[m], phi_t[m]) if t < 2 else (theta_sb[m], theta_t[m])
+                first = 2 * (t % 2)
+                feat_bank = psum_tr.tile([P, HALVES, 2, P], BF16, name="feat_bank", tag="tr")
+            for h in range(HALVES):
+                if live(n):
+                    nc.tensor.matmul(
+                        out=sc_bank[:],
+                        lhsT=theta_t[n][:, h, t * P : (t + 1) * P],
+                        rhs=phi_t[n][:, h, :],
+                        start=(h == 0),
+                        stop=(h == HALVES - 1),
+                    )
+                if live(m):
+                    for s in range(2):
+                        col = (first + s) * FEATURES + h * P
+                        nc.tensor.transpose(feat_bank[:, h, s, :], source[:, col : col + P], ident_bf16[:])
+            if live(m):
+                nc.scalar.copy(
+                    out=target[:, :, first * P : (first + 2) * P],
+                    in_=feat_bank[:].rearrange("a h s r -> a h (s r)"),
+                )
+            if live(n):
+                if t == 0:
+                    neg_max[n] = work.tile([P, QUARTERS], F32, name="neg_max")
+                    exp_sum[n] = work.tile([P, QUARTERS], F32, name="exp_sum")
+                    expo[n] = work.tile([P, QUARTERS, TOKENS], F32, name="expo")
+                nc.vector.tensor_reduce(
+                    out=neg_max[n][:, t : t + 1],
+                    in_=sc_bank[:],
+                    axis=mybir.AxisListType.X,
+                    op=mybir.AluOpType.max,
+                    negate=True,
+                )
+                nc.scalar.activation(
+                    out=expo[n][:, t, :],
+                    in_=sc_bank[:],
+                    func=mybir.ActivationFunctionType.Exp,
+                    bias=neg_max[n][:, t : t + 1],
+                    scale=1.0,
+                    accum_out=exp_sum[n][:, t : t + 1],
+                )
+
+        def normalise(n, c):
+            if c == 0:
+                inv_sum[n] = work.tile([P, QUARTERS], F32, name="inv_sum")
+                nc.vector.reciprocal(out=inv_sum[n][:], in_=exp_sum[n][:])
+                cov_codes[n] = work.tile([P, TOKENS], U32, name="cov_codes", align_bytes=64)
+                cov_scales[n] = work.tile([P, TOKENS], U8, name="cov_scales", align_bytes=64)
+            cov_grouped[n, c] = work.tile([P, P * PACK], BF16, name="cov_grouped", align_bytes=64)
+            nc.vector.tensor_tensor(
+                out=cov_grouped[n, c][:].rearrange("p (i t) -> p i t", t=QUARTERS),
+                in0=expo[n][:, :, c * P : (c + 1) * P].rearrange("p t i -> p i t"),
+                in1=inv_sum[n][:].unsqueeze(1).to_broadcast([P, P, QUARTERS]),
+                op=mybir.AluOpType.mult,
+            )
+
+        def quantise_cov(n, c):
+            cols = slice(c * P, (c + 1) * P)
+            nc.vector.quantize_mx(
+                out=cov_codes[n][:, cols].bitcast(FP8X4), scales=cov_scales[n][:, cols], in_=cov_grouped[n, c][:]
+            )
+
+        def project(n):
+            for h in range(HALVES):
+                x3_bank[n, h] = psum_mx.tile([P, QUARTERS, P], F32, name="x3_bank", tag="mx")
+                for t in range(QUARTERS):
+                    for g in range(PASSES):
+                        rows = slice((t * PASSES + g) * P, (t * PASSES + g + 1) * P)
+                        cols = slice(g * FEATURES + h * P, g * FEATURES + (h + 1) * P)
+                        nc.tensor.matmul_mx(
+                            out=x3_bank[n, h][:, t, :],
+                            lhsT=x_codes[n][:, rows].bitcast(FP8X4),
+                            lhsT_scale=x_scales[n][:, rows],
+                            rhs=w_codes[:, cols].bitcast(FP8X4),
+                            rhs_scale=w_scales[:, cols],
+                            start=(g == 0),
+                            stop=(g == PASSES - 1),
+                        )
+
+        def add_bias(n, h):
+            if h == 0:
+                x3_grouped[n] = work.tile([P, FEATURES * PACK], BF16, name="x3_grouped", align_bytes=64)
+            feats = slice(h * P, (h + 1) * P)
+            nc.vector.tensor_tensor(
+                out=x3_grouped[n][:].rearrange("p (a t) -> p a t", t=QUARTERS)[:, feats, :],
+                in0=x3_bank[n, h][:].rearrange("p t a -> p a t"),
+                in1=bias[:, feats].unsqueeze(2).to_broadcast([P, P, QUARTERS]),
+                op=mybir.AluOpType.add,
+            )
+
+        def quantise_x3(n):
+            x3_codes[n] = work.tile([P, FEATURES], U32, name="x3_codes", align_bytes=64)
+            x3_scales[n] = work.tile([P, FEATURES], U8, name="x3_scales", align_bytes=64)
+            nc.vector.quantize_mx(out=x3_codes[n][:].bitcast(FP8X4), scales=x3_scales[n][:], in_=x3_grouped[n][:])
+
+        def attend_and_store(n):
+            out_sb = work.tile([P, QUARTERS, FEATURES], F32, name="out_sb")
+            for pair in range(QUARTERS // 2):
+                out_bank = psum_mx.tile([P, 2, FEATURES], F32, name="out_bank", tag="mx")
+                for s in range(2):
+                    cols = slice((2 * pair + s) * P, (2 * pair + s + 1) * P)
+                    nc.tensor.matmul_mx(
+                        out=out_bank[:, s, :],
+                        lhsT=cov_codes[n][:, cols].bitcast(FP8X4),
+                        lhsT_scale=cov_scales[n][:, cols],
+                        rhs=x3_codes[n][:].bitcast(FP8X4),
+                        rhs_scale=x3_scales[n][:],
+                        start=True,
+                        stop=True,
+                    )
+                nc.scalar.copy(out=out_sb[:, 2 * pair : 2 * pair + 2, :], in_=out_bank[:])
+            nc.sync.dma_start(out=out[n].rearrange("(p c) a -> p c a", c=QUARTERS), in_=out_sb[:])
+
+        for k in range(-1, SAMPLES + 2):
+            for t in range(QUARTERS):
+                if t == 0 and live(k + 3):
+                    load_sample(k + 3)
+                if live(k + 1):
+                    transpose_x(k + 1, t)
+                scores_and_feature_transposes(k, t)
+                if live(k - 1):
+                    normalise(k - 1, t)
+                if t == 0 and live(k - 1):
+                    quantise_x3(k - 1)
+                if t == 0 and live(k):
+                    quantise_x(k, QUARTERS - 1)
+                if t > 0 and live(k + 1):
+                    quantise_x(k + 1, t - 1)
+                if live(k - 1):
+                    quantise_cov(k - 1, t)
+                if t == 1 and live(k - 2):
+                    attend_and_store(k - 2)
+                if t == 2 and live(k):
+                    project(k)
+                if t == 3 and live(k):
+                    add_bias(k, 0)
+                    add_bias(k, 1)

@@ -12,10 +12,11 @@ FP8X4 = mybir.dt.float8_e4m3fn_x4
 SAMPLES, TOKENS, CHANNELS, FEATURES = 16, 512, 1024, 256
 P = 128
 PACK = 4
+PAIR = 2
 QUARTERS = TOKENS // P
 PASSES = CHANNELS // (P * PACK)
 HALVES = FEATURES // P
-WORDS = CHANNELS // 2
+WORD_BLOCKS = CHANNELS // (P * PAIR)
 
 FLOPS = 2 * SAMPLES * TOKENS * (CHANNELS * FEATURES + 2 * TOKENS * FEATURES)
 
@@ -27,15 +28,17 @@ def tile_vc_interaction_sa_module_pa_t_kernel(tc, x, W_psi, b_psi, x_phi, x_thet
         loads = ctx.enter_context(tc.tile_pool(name="loads", bufs=3))
         work = ctx.enter_context(tc.tile_pool(name="work", bufs=3))
         psum_tr = ctx.enter_context(tc.psum_pool(name="psum_tr", bufs=3))
-        psum_sc = ctx.enter_context(tc.psum_pool(name="psum_sc", bufs=2))
-        psum_mx = ctx.enter_context(tc.psum_pool(name="psum_mx", bufs=3))
+        psum_sc = ctx.enter_context(tc.psum_pool(name="psum_sc", bufs=3))
+        psum_mx = ctx.enter_context(tc.psum_pool(name="psum_mx", bufs=2))
+        ctx.enter_context(tc.manual_schedule())
 
         x_sb, phi_sb, theta_sb = {}, {}, {}
-        x_grouped, x_codes, x_scales = {}, {}, {}
-        phi_t, theta_t = {}, {}
-        neg_max, exp_sum, inv_sum, expo = {}, {}, {}, {}
+        x_bank, x_grouped, x_codes, x_scales = {}, {}, {}, {}
+        feat_bank, phi_t, theta_t = {}, {}, {}
+        sc_bank, neg_max, exp_sum, inv_sum, expo = {}, {}, {}, {}, {}
         cov_grouped, cov_codes, cov_scales = {}, {}, {}
         x3_bank, x3_grouped, x3_codes, x3_scales = {}, {}, {}, {}
+        out_bank, out_sb = {}, {}
 
         def live(n):
             return 0 <= n < SAMPLES
@@ -43,142 +46,61 @@ def tile_vc_interaction_sa_module_pa_t_kernel(tc, x, W_psi, b_psi, x_phi, x_thet
         def by_quarters(rows):
             return rows.rearrange("(p t) w -> p (t w)", t=QUARTERS)
 
+        def words(tile_ap):
+            return tile_ap.bitcast(F32)
+
+        def grouped_read(bank):
+            return bank[:].rearrange("q (g u) r -> q g r u", g=PASSES)
+
         def load_sample(n):
-            x_sb[n] = loads.tile([P, QUARTERS * CHANNELS], BF16, name="x_sb")
-            nc.sync.dma_start(out=x_sb[n][:], in_=by_quarters(x[n]))
+            if not live(n):
+                return
             phi_sb[n] = loads.tile([P, QUARTERS * FEATURES], BF16, name="phi_sb")
             nc.sync.dma_start(out=phi_sb[n][:], in_=by_quarters(x_phi[n]))
             theta_sb[n] = loads.tile([P, QUARTERS * FEATURES], BF16, name="theta_sb")
             nc.sync.dma_start(out=theta_sb[n][:], in_=by_quarters(x_theta[n]))
+            x_sb[n] = loads.tile([P, QUARTERS * CHANNELS], BF16, name="x_sb")
+            nc.sync.dma_start(out=x_sb[n][:], in_=by_quarters(x[n]))
 
-        def transpose_channel_words(words, grouped_words, copy):
-            bank = psum_tr.tile([P, PASSES * 2, P], F32, name="word_bank", tag="tr")
-            for v in range(PASSES * 2):
-                nc.tensor.transpose(bank[:, v, :], words[:, v * P : (v + 1) * P], ident_f32[:])
-            copy(out=grouped_words, in_=bank[:].rearrange("q (g u) r -> q g r u", g=PASSES))
-
-        ident_f32 = consts.tile([P, P], F32, name="ident_f32")
-        make_identity(nc, ident_f32[:])
-        ident_bf16 = consts.tile([P, P], BF16, name="ident_bf16")
-        make_identity(nc, ident_bf16[:])
-
-        w_sb = consts.tile([P, HALVES * CHANNELS], BF16, name="w_sb")
-        nc.sync.dma_start(
-            out=w_sb[:].rearrange("p (h c) -> p h c", h=HALVES),
-            in_=W_psi.rearrange("(h p) c -> p h c", p=P),
-        )
-        load_sample(0)
-        load_sample(1)
-        bias_bf16 = consts.tile([P, FEATURES], BF16, name="bias_bf16")
-        nc.scalar.dma_start(out=bias_bf16[:], in_=b_psi.partition_broadcast(P))
-        bias = consts.tile([P, FEATURES], F32, name="bias")
-        nc.vector.tensor_copy(out=bias[:], in_=bias_bf16[:])
-
-        w_grouped = consts.tile([P, PASSES * FEATURES * PACK], BF16, name="w_grouped", align_bytes=64)
-        w_grouped_words = w_grouped[:].bitcast(F32).rearrange("q (g a u) -> q g a u", g=PASSES, u=2)
-        for h in range(HALVES):
-            transpose_channel_words(
-                w_sb[:].bitcast(F32)[:, h * WORDS : (h + 1) * WORDS],
-                w_grouped_words[:, :, h * P : (h + 1) * P, :],
-                nc.vector.tensor_copy,
-            )
-        w_codes = consts.tile([P, PASSES * FEATURES], U32, name="w_codes", align_bytes=64)
-        w_scales = consts.tile([P, PASSES * FEATURES], U8, name="w_scales", align_bytes=64)
-        nc.vector.quantize_mx(out=w_codes[:].bitcast(FP8X4), scales=w_scales[:], in_=w_grouped[:])
-
-        def transpose_x(n, t):
-            if t == 0:
-                x_codes[n] = work.tile([P, QUARTERS * PASSES * P], U32, name="x_codes", align_bytes=64)
-                x_scales[n] = work.tile([P, QUARTERS * PASSES * P], U8, name="x_scales", align_bytes=64)
-            x_grouped[n, t] = work.tile([P, PASSES * P * PACK], BF16, name="x_grouped", align_bytes=64)
-            transpose_channel_words(
-                x_sb[n][:].bitcast(F32)[:, t * WORDS : (t + 1) * WORDS],
-                x_grouped[n, t][:].bitcast(F32).rearrange("q (g r u) -> q g r u", g=PASSES, u=2),
-                nc.scalar.copy,
-            )
-
-        def quantise_x(n, t):
-            cols = slice(t * PASSES * P, (t + 1) * PASSES * P)
-            nc.vector.quantize_mx(
-                out=x_codes[n][:, cols].bitcast(FP8X4), scales=x_scales[n][:, cols], in_=x_grouped[n, t][:]
-            )
-
-        def scores_and_feature_transposes(n, t):
-            m = n + 1
+        def store_sample(n):
             if live(n):
-                sc_bank = psum_sc.tile([P, TOKENS], F32, name="sc_bank")
+                nc.sync.dma_start(out=by_quarters(out[n]), in_=out_sb[n][:])
+
+        def scores_and_x_transposes(n, t, m, s):
+            if live(n):
+                sc_bank[n, t] = psum_sc.tile([P, TOKENS], F32, name="sc_bank")
             if live(m):
-                if t == 0:
-                    phi_t[m] = work.tile([P, HALVES, TOKENS], BF16, name="phi_t")
-                    theta_t[m] = work.tile([P, HALVES, TOKENS], BF16, name="theta_t")
-                source, target = (phi_sb[m], phi_t[m]) if t < 2 else (theta_sb[m], theta_t[m])
-                first = 2 * (t % 2)
-                feat_bank = psum_tr.tile([P, HALVES, 2, P], BF16, name="feat_bank", tag="tr")
-            for h in range(HALVES):
+                x_bank[m, s] = psum_tr.tile([P, WORD_BLOCKS, P], F32, name="x_bank", tag="tr")
+            for e in range(PAIR):
                 if live(n):
                     nc.tensor.matmul(
-                        out=sc_bank[:],
-                        lhsT=theta_t[n][:, h, t * P : (t + 1) * P],
-                        rhs=phi_t[n][:, h, :],
-                        start=(h == 0),
-                        stop=(h == HALVES - 1),
+                        out=sc_bank[n, t][:],
+                        lhsT=theta_t[n][:, t * P : (t + 1) * P, e],
+                        rhs=phi_t[n][:, :, e],
+                        start=(e == 0),
+                        stop=(e == PAIR - 1),
                     )
                 if live(m):
-                    for s in range(2):
-                        col = (first + s) * FEATURES + h * P
-                        nc.tensor.transpose(feat_bank[:, h, s, :], source[:, col : col + P], ident_bf16[:])
-            if live(m):
-                nc.scalar.copy(
-                    out=target[:, :, first * P : (first + 2) * P],
-                    in_=feat_bank[:].rearrange("a h s r -> a h (s r)"),
-                )
-            if live(n):
-                if t == 0:
-                    neg_max[n] = work.tile([P, QUARTERS], F32, name="neg_max")
-                    exp_sum[n] = work.tile([P, QUARTERS], F32, name="exp_sum")
-                    expo[n] = work.tile([P, QUARTERS, TOKENS], F32, name="expo")
-                nc.vector.tensor_reduce(
-                    out=neg_max[n][:, t : t + 1],
-                    in_=sc_bank[:],
-                    axis=mybir.AxisListType.X,
-                    op=mybir.AluOpType.max,
-                    negate=True,
-                )
-                nc.scalar.activation(
-                    out=expo[n][:, t, :],
-                    in_=sc_bank[:],
-                    func=mybir.ActivationFunctionType.Exp,
-                    bias=neg_max[n][:, t : t + 1],
-                    scale=1.0,
-                    accum_out=exp_sum[n][:, t : t + 1],
-                )
+                    for v in range(e * WORD_BLOCKS // PAIR, (e + 1) * WORD_BLOCKS // PAIR):
+                        col = (s * WORD_BLOCKS + v) * P
+                        nc.tensor.transpose(x_bank[m, s][:, v, :], words(x_sb[m][:])[:, col : col + P], ident[:])
 
-        def normalise(n, c):
-            if c == 0:
-                inv_sum[n] = work.tile([P, QUARTERS], F32, name="inv_sum")
-                nc.vector.reciprocal(out=inv_sum[n][:], in_=exp_sum[n][:])
-                cov_codes[n] = work.tile([P, TOKENS], U32, name="cov_codes", align_bytes=64)
-                cov_scales[n] = work.tile([P, TOKENS], U8, name="cov_scales", align_bytes=64)
-            cov_grouped[n, c] = work.tile([P, P * PACK], BF16, name="cov_grouped", align_bytes=64)
-            nc.vector.tensor_tensor(
-                out=cov_grouped[n, c][:].rearrange("p (i t) -> p i t", t=QUARTERS),
-                in0=expo[n][:, :, c * P : (c + 1) * P].rearrange("p t i -> p i t"),
-                in1=inv_sum[n][:].unsqueeze(1).to_broadcast([P, P, QUARTERS]),
-                op=mybir.AluOpType.mult,
-            )
-
-        def quantise_cov(n, c):
-            cols = slice(c * P, (c + 1) * P)
-            nc.vector.quantize_mx(
-                out=cov_codes[n][:, cols].bitcast(FP8X4), scales=cov_scales[n][:, cols], in_=cov_grouped[n, c][:]
-            )
+        def transpose_features(source, n):
+            if not live(n):
+                return
+            feat_bank[n] = psum_tr.tile([P, QUARTERS, P], F32, name="feat_bank", tag="tr")
+            for t in range(QUARTERS):
+                nc.tensor.transpose(feat_bank[n][:, t, :], words(source[n][:])[:, t * P : (t + 1) * P], ident[:])
 
         def project(n):
+            if not live(n):
+                return
             for h in range(HALVES):
                 x3_bank[n, h] = psum_mx.tile([P, QUARTERS, P], F32, name="x3_bank", tag="mx")
-                for t in range(QUARTERS):
-                    for g in range(PASSES):
-                        rows = slice((t * PASSES + g) * P, (t * PASSES + g + 1) * P)
+            for t in range(QUARTERS):
+                for g in range(PASSES):
+                    rows = slice((t * PASSES + g) * P, (t * PASSES + g + 1) * P)
+                    for h in range(HALVES):
                         cols = slice(g * FEATURES + h * P, g * FEATURES + (h + 1) * P)
                         nc.tensor.matmul_mx(
                             out=x3_bank[n, h][:, t, :],
@@ -190,61 +112,198 @@ def tile_vc_interaction_sa_module_pa_t_kernel(tc, x, W_psi, b_psi, x_phi, x_thet
                             stop=(g == PASSES - 1),
                         )
 
-        def add_bias(n, h):
-            if h == 0:
-                x3_grouped[n] = work.tile([P, FEATURES * PACK], BF16, name="x3_grouped", align_bytes=64)
-            feats = slice(h * P, (h + 1) * P)
-            nc.vector.tensor_tensor(
-                out=x3_grouped[n][:].rearrange("p (a t) -> p a t", t=QUARTERS)[:, feats, :],
-                in0=x3_bank[n, h][:].rearrange("p t a -> p a t"),
-                in1=bias[:, feats].unsqueeze(2).to_broadcast([P, P, QUARTERS]),
-                op=mybir.AluOpType.add,
+        def attend(n):
+            if not live(n):
+                return
+            for c in range(QUARTERS):
+                if c % 2 == 0:
+                    out_bank[n, c // 2] = psum_mx.tile([P, 2, FEATURES], F32, name="out_bank", tag="mx")
+                cols = slice(c * P, (c + 1) * P)
+                nc.tensor.matmul_mx(
+                    out=out_bank[n, c // 2][:, c % 2, :],
+                    lhsT=cov_codes[n][:, cols].bitcast(FP8X4),
+                    lhsT_scale=cov_scales[n][:, cols],
+                    rhs=x3_codes[n][:].bitcast(FP8X4),
+                    rhs_scale=x3_scales[n][:],
+                    start=True,
+                    stop=True,
+                )
+
+        def group_x(n, t):
+            if not live(n):
+                return
+            x_grouped[n, t] = work.tile([P, PASSES * P * PACK], BF16, name="x_grouped", align_bytes=64)
+            nc.scalar.copy(
+                out=words(x_grouped[n, t][:]).rearrange("q (g r u) -> q g r u", g=PASSES, u=PAIR),
+                in_=grouped_read(x_bank[n, t]),
             )
 
+        def keep_features(target, name, n):
+            if not live(n):
+                return
+            target[n] = work.tile([P, TOKENS, PAIR], BF16, name=name)
+            nc.scalar.copy(
+                out=words(target[n][:].rearrange("q r e -> q (r e)")),
+                in_=feat_bank[n][:].rearrange("q t r -> q (t r)"),
+            )
+
+        def exponentials(n, t):
+            if not live(n):
+                return
+            if t == 0:
+                exp_sum[n] = work.tile([P, QUARTERS], F32, name="exp_sum")
+                expo[n] = work.tile([P, QUARTERS, TOKENS], F32, name="expo")
+            nc.scalar.activation(
+                out=expo[n][:, t, :],
+                in_=sc_bank[n, t][:],
+                func=mybir.ActivationFunctionType.Exp,
+                bias=neg_max[n][:, t : t + 1],
+                scale=1.0,
+                accum_out=exp_sum[n][:, t : t + 1],
+            )
+
+        def fetch_out(n):
+            if not live(n):
+                return
+            out_sb[n] = work.tile([P, QUARTERS * FEATURES], F32, name="out_sb")
+            for b in range(QUARTERS // 2):
+                nc.scalar.copy(
+                    out=out_sb[n][:, 2 * b * FEATURES : 2 * (b + 1) * FEATURES],
+                    in_=out_bank[n, b][:].rearrange("p c a -> p (c a)"),
+                )
+
+        def maximum(n, t):
+            if not live(n):
+                return
+            if t == 0:
+                neg_max[n] = work.tile([P, QUARTERS], F32, name="neg_max")
+            nc.vector.tensor_reduce(
+                out=neg_max[n][:, t : t + 1],
+                in_=sc_bank[n, t][:],
+                axis=mybir.AxisListType.X,
+                op=mybir.AluOpType.max,
+                negate=True,
+            )
+
+        def quantise_x(n, t):
+            if not live(n):
+                return
+            if t == 0:
+                x_codes[n] = work.tile([P, QUARTERS * PASSES * P], U32, name="x_codes", align_bytes=64)
+                x_scales[n] = work.tile([P, QUARTERS * PASSES * P], U8, name="x_scales", align_bytes=64)
+            cols = slice(t * PASSES * P, (t + 1) * PASSES * P)
+            nc.vector.quantize_mx(
+                out=x_codes[n][:, cols].bitcast(FP8X4), scales=x_scales[n][:, cols], in_=x_grouped[n, t][:]
+            )
+
+        def add_bias(n):
+            if not live(n):
+                return
+            x3_grouped[n] = work.tile([P, FEATURES * PACK], BF16, name="x3_grouped", align_bytes=64)
+            for h in range(HALVES):
+                feats = slice(h * P, (h + 1) * P)
+                nc.vector.tensor_tensor(
+                    out=x3_grouped[n][:].rearrange("p (a t) -> p a t", t=QUARTERS)[:, feats, :],
+                    in0=x3_bank[n, h][:].rearrange("p t a -> p a t"),
+                    in1=bias[:, feats].unsqueeze(2).to_broadcast([P, P, QUARTERS]),
+                    op=mybir.AluOpType.add,
+                )
+
         def quantise_x3(n):
+            if not live(n):
+                return
             x3_codes[n] = work.tile([P, FEATURES], U32, name="x3_codes", align_bytes=64)
             x3_scales[n] = work.tile([P, FEATURES], U8, name="x3_scales", align_bytes=64)
             nc.vector.quantize_mx(out=x3_codes[n][:].bitcast(FP8X4), scales=x3_scales[n][:], in_=x3_grouped[n][:])
 
-        def attend_and_store(n):
-            out_sb = work.tile([P, QUARTERS, FEATURES], F32, name="out_sb")
-            for pair in range(QUARTERS // 2):
-                out_bank = psum_mx.tile([P, 2, FEATURES], F32, name="out_bank", tag="mx")
-                for s in range(2):
-                    cols = slice((2 * pair + s) * P, (2 * pair + s + 1) * P)
-                    nc.tensor.matmul_mx(
-                        out=out_bank[:, s, :],
-                        lhsT=cov_codes[n][:, cols].bitcast(FP8X4),
-                        lhsT_scale=cov_scales[n][:, cols],
-                        rhs=x3_codes[n][:].bitcast(FP8X4),
-                        rhs_scale=x3_scales[n][:],
-                        start=True,
-                        stop=True,
-                    )
-                nc.scalar.copy(out=out_sb[:, 2 * pair : 2 * pair + 2, :], in_=out_bank[:])
-            nc.sync.dma_start(out=out[n].rearrange("(p c) a -> p c a", c=QUARTERS), in_=out_sb[:])
+        def reciprocal_of_sums(n):
+            if not live(n):
+                return
+            inv_sum[n] = work.tile([P, QUARTERS], F32, name="inv_sum")
+            nc.vector.reciprocal(out=inv_sum[n][:], in_=exp_sum[n][:])
 
-        for k in range(-1, SAMPLES + 2):
-            for t in range(QUARTERS):
-                if t == 0 and live(k + 3):
-                    load_sample(k + 3)
-                if live(k + 1):
-                    transpose_x(k + 1, t)
-                scores_and_feature_transposes(k, t)
-                if live(k - 1):
-                    normalise(k - 1, t)
-                if t == 0 and live(k - 1):
-                    quantise_x3(k - 1)
-                if t == 0 and live(k):
-                    quantise_x(k, QUARTERS - 1)
-                if t > 0 and live(k + 1):
-                    quantise_x(k + 1, t - 1)
-                if live(k - 1):
-                    quantise_cov(k - 1, t)
-                if t == 1 and live(k - 2):
-                    attend_and_store(k - 2)
-                if t == 2 and live(k):
-                    project(k)
-                if t == 3 and live(k):
-                    add_bias(k, 0)
-                    add_bias(k, 1)
+        def normalise(n, c):
+            if not live(n):
+                return
+            cov_grouped[n, c] = work.tile([P, P * PACK], BF16, name="cov_grouped", align_bytes=64)
+            nc.vector.tensor_tensor(
+                out=cov_grouped[n, c][:].rearrange("p (i t) -> p i t", t=QUARTERS),
+                in0=expo[n][:, :, c * P : (c + 1) * P].rearrange("p t i -> p i t"),
+                in1=inv_sum[n][:].unsqueeze(1).to_broadcast([P, P, QUARTERS]),
+                op=mybir.AluOpType.mult,
+            )
+
+        def quantise_cov(n, c):
+            if not live(n):
+                return
+            if c == 0:
+                cov_codes[n] = work.tile([P, TOKENS], U32, name="cov_codes", align_bytes=64)
+                cov_scales[n] = work.tile([P, TOKENS], U8, name="cov_scales", align_bytes=64)
+            cols = slice(c * P, (c + 1) * P)
+            nc.vector.quantize_mx(
+                out=cov_codes[n][:, cols].bitcast(FP8X4), scales=cov_scales[n][:, cols], in_=cov_grouped[n, c][:]
+            )
+
+        ident = consts.tile([P, P], F32, name="ident")
+        make_identity(nc, ident[:])
+        w_sb = consts.tile([P, HALVES * CHANNELS], BF16, name="w_sb")
+        nc.sync.dma_start(
+            out=w_sb[:].rearrange("p (h c) -> p h c", h=HALVES),
+            in_=W_psi.rearrange("(h p) c -> p h c", p=P),
+        )
+        load_sample(0)
+        load_sample(1)
+        bias = consts.tile([P, FEATURES], BF16, name="bias")
+        nc.scalar.dma_start(out=bias[:], in_=b_psi.partition_broadcast(P))
+
+        w_grouped = consts.tile([P, PASSES * FEATURES * PACK], BF16, name="w_grouped", align_bytes=64)
+        for h in range(HALVES):
+            w_bank = psum_tr.tile([P, WORD_BLOCKS, P], F32, name="w_bank", tag="tr")
+            for v in range(WORD_BLOCKS):
+                col = (h * WORD_BLOCKS + v) * P
+                nc.tensor.transpose(w_bank[:, v, :], words(w_sb[:])[:, col : col + P], ident[:])
+            nc.vector.tensor_copy(
+                out=words(w_grouped[:]).rearrange("q (g a u) -> q g a u", g=PASSES, u=PAIR)[:, :, h * P : (h + 1) * P, :],
+                in_=grouped_read(w_bank),
+            )
+        w_codes = consts.tile([P, PASSES * FEATURES], U32, name="w_codes", align_bytes=64)
+        w_scales = consts.tile([P, PASSES * FEATURES], U8, name="w_scales", align_bytes=64)
+        nc.vector.quantize_mx(out=w_codes[:].bitcast(FP8X4), scales=w_scales[:], in_=w_grouped[:])
+
+        for step in range(-QUARTERS, QUARTERS * SAMPLES + 9):
+            n, t = divmod(step, QUARTERS)
+
+            if t == 0:
+                store_sample(n - 3)
+            if t == 2:
+                load_sample(n + 3)
+
+            group_x(*divmod(step + 1, QUARTERS))
+            if t == 1:
+                keep_features(phi_t, "phi_t", n + 1)
+            if t == 2:
+                keep_features(theta_t, "theta_t", n + 1)
+            exponentials(*divmod(step - 2, QUARTERS))
+            if t == 3:
+                fetch_out(n - 2)
+
+            if t == 2:
+                reciprocal_of_sums(n - 1)
+            maximum(*divmod(step - 1, QUARTERS))
+            normalise(*divmod(step - 6, QUARTERS))
+            quantise_x(n, t)
+            quantise_cov(*divmod(step - 6, QUARTERS))
+            if t == 1:
+                add_bias(n - 1)
+            if t == 2:
+                quantise_x3(n - 1)
+
+            scores_and_x_transposes(n, t, *divmod(step + 2, QUARTERS))
+            if t == 0:
+                transpose_features(phi_sb, n + 1)
+            if t == 1:
+                transpose_features(theta_sb, n + 1)
+            if t == 0:
+                project(n - 1)
+            if t == 2:
+                attend(n - 2)

@@ -132,9 +132,10 @@ def tile_vc_interaction_sa_module_pa_t_kernel(tc, x, W_psi, b_psi, x_phi, x_thet
         def group_x(n, t):
             if not live(n):
                 return
-            x_grouped[n, t] = work.tile([P, PASSES * P * PACK], BF16, name="x_grouped", align_bytes=64)
+            if t == 0:
+                x_grouped[n] = work.tile([P, QUARTERS, PASSES * P * PACK], BF16, name="x_grouped", align_bytes=64)
             nc.scalar.copy(
-                out=words(x_grouped[n, t][:]).rearrange("q (g r u) -> q g r u", g=PASSES, u=PAIR),
+                out=words(x_grouped[n][:, t, :]).rearrange("q (g r u) -> q g r u", g=PASSES, u=PAIR),
                 in_=grouped_read(x_bank[n, t]),
             )
 
@@ -185,15 +186,15 @@ def tile_vc_interaction_sa_module_pa_t_kernel(tc, x, W_psi, b_psi, x_phi, x_thet
                 negate=True,
             )
 
-        def quantise_x(n, t):
+        def quantise_x(n):
             if not live(n):
                 return
-            if t == 0:
-                x_codes[n] = work.tile([P, QUARTERS * PASSES * P], U32, name="x_codes", align_bytes=64)
-                x_scales[n] = work.tile([P, QUARTERS * PASSES * P], U8, name="x_scales", align_bytes=64)
-            cols = slice(t * PASSES * P, (t + 1) * PASSES * P)
+            x_codes[n] = work.tile([P, QUARTERS * PASSES * P], U32, name="x_codes", align_bytes=64)
+            x_scales[n] = work.tile([P, QUARTERS * PASSES * P], U8, name="x_scales", align_bytes=64)
             nc.vector.quantize_mx(
-                out=x_codes[n][:, cols].bitcast(FP8X4), scales=x_scales[n][:, cols], in_=x_grouped[n, t][:]
+                out=x_codes[n][:].bitcast(FP8X4),
+                scales=x_scales[n][:],
+                in_=x_grouped[n][:].rearrange("q t w -> q (t w)"),
             )
 
         def add_bias(n):
@@ -222,27 +223,23 @@ def tile_vc_interaction_sa_module_pa_t_kernel(tc, x, W_psi, b_psi, x_phi, x_thet
             inv_sum[n] = work.tile([P, QUARTERS], F32, name="inv_sum")
             nc.vector.reciprocal(out=inv_sum[n][:], in_=exp_sum[n][:])
 
-        def normalise(n, c):
+        def normalise(n):
             if not live(n):
                 return
-            cov_grouped[n, c] = work.tile([P, P * PACK], BF16, name="cov_grouped", align_bytes=64)
+            cov_grouped[n] = work.tile([P, TOKENS * PACK], BF16, name="cov_grouped", align_bytes=64)
             nc.vector.tensor_tensor(
-                out=cov_grouped[n, c][:].rearrange("p (i t) -> p i t", t=QUARTERS),
-                in0=expo[n][:, :, c * P : (c + 1) * P].rearrange("p t i -> p i t"),
-                in1=inv_sum[n][:].unsqueeze(1).to_broadcast([P, P, QUARTERS]),
+                out=cov_grouped[n][:].rearrange("p (i t) -> p i t", t=QUARTERS),
+                in0=expo[n][:].rearrange("p t i -> p i t"),
+                in1=inv_sum[n][:].unsqueeze(1).to_broadcast([P, TOKENS, QUARTERS]),
                 op=mybir.AluOpType.mult,
             )
 
-        def quantise_cov(n, c):
+        def quantise_cov(n):
             if not live(n):
                 return
-            if c == 0:
-                cov_codes[n] = work.tile([P, TOKENS], U32, name="cov_codes", align_bytes=64)
-                cov_scales[n] = work.tile([P, TOKENS], U8, name="cov_scales", align_bytes=64)
-            cols = slice(c * P, (c + 1) * P)
-            nc.vector.quantize_mx(
-                out=cov_codes[n][:, cols].bitcast(FP8X4), scales=cov_scales[n][:, cols], in_=cov_grouped[n, c][:]
-            )
+            cov_codes[n] = work.tile([P, TOKENS], U32, name="cov_codes", align_bytes=64)
+            cov_scales[n] = work.tile([P, TOKENS], U8, name="cov_scales", align_bytes=64)
+            nc.vector.quantize_mx(out=cov_codes[n][:].bitcast(FP8X4), scales=cov_scales[n][:], in_=cov_grouped[n][:])
 
         ident = consts.tile([P, P], F32, name="ident")
         make_identity(nc, ident[:])
@@ -278,7 +275,7 @@ def tile_vc_interaction_sa_module_pa_t_kernel(tc, x, W_psi, b_psi, x_phi, x_thet
             if t == 2:
                 load_sample(n + 3)
 
-            group_x(*divmod(step + 1, QUARTERS))
+            group_x(*divmod(step + 2, QUARTERS))
             if t == 1:
                 keep_features(phi_t, "phi_t", n + 1)
             if t == 2:
@@ -290,15 +287,17 @@ def tile_vc_interaction_sa_module_pa_t_kernel(tc, x, W_psi, b_psi, x_phi, x_thet
             if t == 2:
                 reciprocal_of_sums(n - 1)
             maximum(*divmod(step - 1, QUARTERS))
-            normalise(*divmod(step - 6, QUARTERS))
-            quantise_x(n, t)
-            quantise_cov(*divmod(step - 6, QUARTERS))
+            if t == 0:
+                quantise_cov(n - 2)
             if t == 1:
                 add_bias(n - 1)
             if t == 2:
+                quantise_x(n)
                 quantise_x3(n - 1)
+            if t == 3:
+                normalise(n - 1)
 
-            scores_and_x_transposes(n, t, *divmod(step + 2, QUARTERS))
+            scores_and_x_transposes(n, t, *divmod(step + 3, QUARTERS))
             if t == 0:
                 transpose_features(phi_sb, n + 1)
             if t == 1:

@@ -17,6 +17,7 @@ QUARTERS = TOKENS // P
 PASSES = CHANNELS // (P * PACK)
 HALVES = FEATURES // P
 WORD_BLOCKS = CHANNELS // (P * PAIR)
+RUN = 4
 
 FLOPS = 2 * SAMPLES * TOKENS * (CHANNELS * FEATURES + 2 * TOKENS * FEATURES)
 
@@ -228,9 +229,9 @@ def tile_vc_interaction_sa_module_pa_t_kernel(tc, x, W_psi, b_psi, x_phi, x_thet
                 return
             cov_grouped[n] = work.tile([P, TOKENS * PACK], BF16, name="cov_grouped", align_bytes=64)
             nc.vector.tensor_tensor(
-                out=cov_grouped[n][:].rearrange("p (i t) -> p i t", t=QUARTERS),
-                in0=expo[n][:].rearrange("p t i -> p i t"),
-                in1=inv_sum[n][:].unsqueeze(1).to_broadcast([P, TOKENS, QUARTERS]),
+                out=cov_grouped[n][:].rearrange("p (c i t) -> p c t i", i=RUN, t=QUARTERS),
+                in0=expo[n][:].rearrange("p t (c i) -> p c t i", i=RUN),
+                in1=inv_sum[n][:].unsqueeze(1).unsqueeze(3).to_broadcast([P, TOKENS // RUN, QUARTERS, RUN]),
                 op=mybir.AluOpType.mult,
             )
 

@@ -18,6 +18,8 @@ PASSES = CHANNELS // (P * PACK)
 HALVES = FEATURES // P
 WORD_BLOCKS = CHANNELS // (P * PAIR)
 RUN = 4
+GPSIMD_COLUMNS = 192
+VECTOR_COLUMNS = TOKENS - GPSIMD_COLUMNS
 
 FLOPS = 2 * SAMPLES * TOKENS * (CHANNELS * FEATURES + 2 * TOKENS * FEATURES)
 
@@ -224,14 +226,24 @@ def tile_vc_interaction_sa_module_pa_t_kernel(tc, x, W_psi, b_psi, x_phi, x_thet
             inv_sum[n] = work.tile([P, QUARTERS], F32, name="inv_sum")
             nc.vector.reciprocal(out=inv_sum[n][:], in_=exp_sum[n][:])
 
-        def normalise(n):
+        def normalise_on_gpsimd(n):
             if not live(n):
                 return
             cov_grouped[n] = work.tile([P, TOKENS * PACK], BF16, name="cov_grouped", align_bytes=64)
+            nc.gpsimd.tensor_tensor(
+                out=cov_grouped[n][:, VECTOR_COLUMNS * PACK :].rearrange("p (i t) -> p i t", t=QUARTERS),
+                in0=expo[n][:, :, VECTOR_COLUMNS:].rearrange("p t i -> p i t"),
+                in1=inv_sum[n][:].unsqueeze(1).to_broadcast([P, GPSIMD_COLUMNS, QUARTERS]),
+                op=mybir.AluOpType.mult,
+            )
+
+        def normalise_on_vector(n):
+            if not live(n):
+                return
             nc.vector.tensor_tensor(
-                out=cov_grouped[n][:].rearrange("p (c i t) -> p c t i", i=RUN, t=QUARTERS),
-                in0=expo[n][:].rearrange("p t (c i) -> p c t i", i=RUN),
-                in1=inv_sum[n][:].unsqueeze(1).unsqueeze(3).to_broadcast([P, TOKENS // RUN, QUARTERS, RUN]),
+                out=cov_grouped[n][:, : VECTOR_COLUMNS * PACK].rearrange("p (c i t) -> p c t i", i=RUN, t=QUARTERS),
+                in0=expo[n][:, :, :VECTOR_COLUMNS].rearrange("p t (c i) -> p c t i", i=RUN),
+                in1=inv_sum[n][:].unsqueeze(1).unsqueeze(3).to_broadcast([P, VECTOR_COLUMNS // RUN, QUARTERS, RUN]),
                 op=mybir.AluOpType.mult,
             )
 
@@ -268,42 +280,43 @@ def tile_vc_interaction_sa_module_pa_t_kernel(tc, x, W_psi, b_psi, x_phi, x_thet
         w_scales = consts.tile([P, PASSES * FEATURES], U8, name="w_scales", align_bytes=64)
         nc.vector.quantize_mx(out=w_codes[:].bitcast(FP8X4), scales=w_scales[:], in_=w_grouped[:])
 
-        for step in range(-QUARTERS, QUARTERS * SAMPLES + 9):
+        for step in range(-QUARTERS, QUARTERS * SAMPLES + 10):
             n, t = divmod(step, QUARTERS)
 
-            if t == 0:
+            if t == 1:
                 store_sample(n - 3)
             if t == 2:
                 load_sample(n + 3)
 
-            group_x(*divmod(step + 2, QUARTERS))
+            group_x(*divmod(step + 1, QUARTERS))
             if t == 1:
                 keep_features(phi_t, "phi_t", n + 1)
             if t == 2:
                 keep_features(theta_t, "theta_t", n + 1)
             exponentials(*divmod(step - 2, QUARTERS))
-            if t == 3:
-                fetch_out(n - 2)
+            if t == 0:
+                fetch_out(n - 3)
 
             if t == 2:
                 reciprocal_of_sums(n - 1)
+                normalise_on_gpsimd(n - 1)
             maximum(*divmod(step - 1, QUARTERS))
             if t == 0:
-                quantise_cov(n - 2)
+                normalise_on_vector(n - 2)
             if t == 1:
-                add_bias(n - 1)
+                quantise_cov(n - 2)
             if t == 2:
+                add_bias(n - 1)
+            if t == 3:
                 quantise_x(n)
                 quantise_x3(n - 1)
-            if t == 3:
-                normalise(n - 1)
 
-            scores_and_x_transposes(n, t, *divmod(step + 3, QUARTERS))
+            scores_and_x_transposes(n, t, *divmod(step + 2, QUARTERS))
             if t == 0:
                 transpose_features(phi_sb, n + 1)
             if t == 1:
                 transpose_features(theta_sb, n + 1)
-            if t == 0:
+            if t == 1:
                 project(n - 1)
-            if t == 2:
+            if t == 3:
                 attend(n - 2)

@@ -18,7 +18,7 @@ PASSES = CHANNELS // (P * PACK)
 HALVES = FEATURES // P
 WORD_BLOCKS = CHANNELS // (P * PAIR)
 RUN = 4
-GPSIMD_COLUMNS = 192
+GPSIMD_COLUMNS = 256
 VECTOR_COLUMNS = TOKENS - GPSIMD_COLUMNS
 
 FLOPS = 2 * SAMPLES * TOKENS * (CHANNELS * FEATURES + 2 * TOKENS * FEATURES)
@@ -291,7 +291,7 @@ def tile_vc_interaction_sa_module_pa_t_kernel(tc, x, W_psi, b_psi, x_phi, x_thet
             group_x(*divmod(step + 1, QUARTERS))
             if t == 1:
                 keep_features(phi_t, "phi_t", n + 1)
-            if t == 2:
+            if t == 3:
                 keep_features(theta_t, "theta_t", n + 1)
             exponentials(*divmod(step - 2, QUARTERS))
             if t == 0:
@@ -302,19 +302,18 @@ def tile_vc_interaction_sa_module_pa_t_kernel(tc, x, W_psi, b_psi, x_phi, x_thet
                 normalise_on_gpsimd(n - 1)
             maximum(*divmod(step - 1, QUARTERS))
             if t == 0:
-                normalise_on_vector(n - 2)
+                quantise_x(n - 1)
             if t == 1:
+                normalise_on_vector(n - 2)
+                quantise_x3(n - 2)
                 quantise_cov(n - 2)
             if t == 2:
                 add_bias(n - 1)
-            if t == 3:
-                quantise_x(n)
-                quantise_x3(n - 1)
 
             scores_and_x_transposes(n, t, *divmod(step + 2, QUARTERS))
             if t == 0:
                 transpose_features(phi_sb, n + 1)
-            if t == 1:
+            if t == 2:
                 transpose_features(theta_sb, n + 1)
             if t == 1:
                 project(n - 1)

@@ -18,8 +18,18 @@ PASSES = CHANNELS // (P * PACK)
 HALVES = FEATURES // P
 WORD_BLOCKS = CHANNELS // (P * PAIR)
 RUN = 4
-GPSIMD_COLUMNS = 256
-VECTOR_COLUMNS = TOKENS - GPSIMD_COLUMNS
+GP = 256
+TR_BANKS, SC_BANKS, MX_BANKS = 3, 3, 2
+X_PIECES = {0: 4}
+
+
+def group_on_vector(n, t):
+    return False
+
+
+def fetch_on_vector(n, b):
+    return n == SAMPLES - 1 and b == 1
+
 
 FLOPS = 2 * SAMPLES * TOKENS * (CHANNELS * FEATURES + 2 * TOKENS * FEATURES)
 
@@ -28,11 +38,11 @@ def tile_vc_interaction_sa_module_pa_t_kernel(tc, x, W_psi, b_psi, x_phi, x_thet
     nc = tc.nc
     with ExitStack() as ctx:
         consts = ctx.enter_context(tc.tile_pool(name="consts", bufs=1))
-        loads = ctx.enter_context(tc.tile_pool(name="loads", bufs=3))
+        loads = ctx.enter_context(tc.tile_pool(name="loads", bufs=4))
         work = ctx.enter_context(tc.tile_pool(name="work", bufs=3))
-        psum_tr = ctx.enter_context(tc.psum_pool(name="psum_tr", bufs=3))
-        psum_sc = ctx.enter_context(tc.psum_pool(name="psum_sc", bufs=3))
-        psum_mx = ctx.enter_context(tc.psum_pool(name="psum_mx", bufs=2))
+        psum_tr = ctx.enter_context(tc.psum_pool(name="psum_tr", bufs=TR_BANKS))
+        psum_sc = ctx.enter_context(tc.psum_pool(name="psum_sc", bufs=SC_BANKS))
+        psum_mx = ctx.enter_context(tc.psum_pool(name="psum_mx", bufs=MX_BANKS))
         ctx.enter_context(tc.manual_schedule())
 
         x_sb, phi_sb, theta_sb = {}, {}, {}
@@ -43,9 +53,6 @@ def tile_vc_interaction_sa_module_pa_t_kernel(tc, x, W_psi, b_psi, x_phi, x_thet
         x3_bank, x3_grouped, x3_codes, x3_scales = {}, {}, {}, {}
         out_bank, out_sb = {}, {}
 
-        def live(n):
-            return 0 <= n < SAMPLES
-
         def by_quarters(rows):
             return rows.rearrange("(p t) w -> p (t w)", t=QUARTERS)
 
@@ -55,55 +62,56 @@ def tile_vc_interaction_sa_module_pa_t_kernel(tc, x, W_psi, b_psi, x_phi, x_thet
         def grouped_read(bank):
             return bank[:].rearrange("q (g u) r -> q g r u", g=PASSES)
 
-        def load_sample(n):
-            if not live(n):
-                return
+        def load_features(n):
             phi_sb[n] = loads.tile([P, QUARTERS * FEATURES], BF16, name="phi_sb")
             nc.sync.dma_start(out=phi_sb[n][:], in_=by_quarters(x_phi[n]))
             theta_sb[n] = loads.tile([P, QUARTERS * FEATURES], BF16, name="theta_sb")
             nc.sync.dma_start(out=theta_sb[n][:], in_=by_quarters(x_theta[n]))
+
+        def load_x(n):
+            pieces = X_PIECES.get(n, 1)
+            wide = QUARTERS * CHANNELS // pieces
             x_sb[n] = loads.tile([P, QUARTERS * CHANNELS], BF16, name="x_sb")
-            nc.sync.dma_start(out=x_sb[n][:], in_=by_quarters(x[n]))
+            for c in range(pieces):
+                cols = slice(c * wide, (c + 1) * wide)
+                nc.sync.dma_start(out=x_sb[n][:, cols], in_=by_quarters(x[n])[:, cols])
 
-        def store_sample(n):
-            if live(n):
-                nc.sync.dma_start(out=by_quarters(out[n]), in_=out_sb[n][:])
+        def store(n, b):
+            cols = slice(2 * b * FEATURES, 2 * (b + 1) * FEATURES)
+            nc.sync.dma_start(out=by_quarters(out[n])[:, cols], in_=out_sb[n][:, cols])
 
-        def scores_and_x_transposes(n, t, m, s):
-            if live(n):
+        def store_all(n):
+            nc.sync.dma_start(out=by_quarters(out[n]), in_=out_sb[n][:])
+
+        def scores(n, t, e):
+            if e == 0:
                 sc_bank[n, t] = psum_sc.tile([P, TOKENS], F32, name="sc_bank")
-            if live(m):
-                x_bank[m, s] = psum_tr.tile([P, WORD_BLOCKS, P], F32, name="x_bank", tag="tr")
-            for e in range(PAIR):
-                if live(n):
-                    nc.tensor.matmul(
-                        out=sc_bank[n, t][:],
-                        lhsT=theta_t[n][:, t * P : (t + 1) * P, e],
-                        rhs=phi_t[n][:, :, e],
-                        start=(e == 0),
-                        stop=(e == PAIR - 1),
-                    )
-                if live(m):
-                    for v in range(e * WORD_BLOCKS // PAIR, (e + 1) * WORD_BLOCKS // PAIR):
-                        col = (s * WORD_BLOCKS + v) * P
-                        nc.tensor.transpose(x_bank[m, s][:, v, :], words(x_sb[m][:])[:, col : col + P], ident[:])
+            nc.tensor.matmul(
+                out=sc_bank[n, t][:],
+                lhsT=theta_t[n][:, t * P : (t + 1) * P, e],
+                rhs=phi_t[n][:, :, e],
+                start=(e == 0),
+                stop=(e == PAIR - 1),
+            )
+
+        def transpose_x(n, s, half):
+            if half == 0:
+                x_bank[n, s] = psum_tr.tile([P, WORD_BLOCKS, P], F32, name="x_bank", tag="tr")
+            for v in range(half * WORD_BLOCKS // 2, (half + 1) * WORD_BLOCKS // 2):
+                col = (s * WORD_BLOCKS + v) * P
+                nc.tensor.transpose(x_bank[n, s][:, v, :], words(x_sb[n][:])[:, col : col + P], ident[:])
 
         def transpose_features(source, n):
-            if not live(n):
-                return
             feat_bank[n] = psum_tr.tile([P, QUARTERS, P], F32, name="feat_bank", tag="tr")
             for t in range(QUARTERS):
                 nc.tensor.transpose(feat_bank[n][:, t, :], words(source[n][:])[:, t * P : (t + 1) * P], ident[:])
 
         def project(n):
-            if not live(n):
-                return
             for h in range(HALVES):
                 x3_bank[n, h] = psum_mx.tile([P, QUARTERS, P], F32, name="x3_bank", tag="mx")
-            for t in range(QUARTERS):
-                for g in range(PASSES):
-                    rows = slice((t * PASSES + g) * P, (t * PASSES + g + 1) * P)
-                    for h in range(HALVES):
+                for t in range(QUARTERS):
+                    for g in range(PASSES):
+                        rows = slice((t * PASSES + g) * P, (t * PASSES + g + 1) * P)
                         cols = slice(g * FEATURES + h * P, g * FEATURES + (h + 1) * P)
                         nc.tensor.matmul_mx(
                             out=x3_bank[n, h][:, t, :],
@@ -115,15 +123,12 @@ def tile_vc_interaction_sa_module_pa_t_kernel(tc, x, W_psi, b_psi, x_phi, x_thet
                             stop=(g == PASSES - 1),
                         )
 
-        def attend(n):
-            if not live(n):
-                return
-            for c in range(QUARTERS):
-                if c % 2 == 0:
-                    out_bank[n, c // 2] = psum_mx.tile([P, 2, FEATURES], F32, name="out_bank", tag="mx")
-                cols = slice(c * P, (c + 1) * P)
+        def attend(n, b):
+            out_bank[n, b] = psum_mx.tile([P, 2, FEATURES], F32, name="out_bank", tag="mx")
+            for c in range(2):
+                cols = slice((2 * b + c) * P, (2 * b + c + 1) * P)
                 nc.tensor.matmul_mx(
-                    out=out_bank[n, c // 2][:, c % 2, :],
+                    out=out_bank[n, b][:, c, :],
                     lhsT=cov_codes[n][:, cols].bitcast(FP8X4),
                     lhsT_scale=cov_scales[n][:, cols],
                     rhs=x3_codes[n][:].bitcast(FP8X4),
@@ -133,18 +138,15 @@ def tile_vc_interaction_sa_module_pa_t_kernel(tc, x, W_psi, b_psi, x_phi, x_thet
                 )
 
         def group_x(n, t):
-            if not live(n):
-                return
             if t == 0:
                 x_grouped[n] = work.tile([P, QUARTERS, PASSES * P * PACK], BF16, name="x_grouped", align_bytes=64)
-            nc.scalar.copy(
+            copy = nc.vector.tensor_copy if group_on_vector(n, t) else nc.scalar.copy
+            copy(
                 out=words(x_grouped[n][:, t, :]).rearrange("q (g r u) -> q g r u", g=PASSES, u=PAIR),
                 in_=grouped_read(x_bank[n, t]),
             )
 
         def keep_features(target, name, n):
-            if not live(n):
-                return
             target[n] = work.tile([P, TOKENS, PAIR], BF16, name=name)
             nc.scalar.copy(
                 out=words(target[n][:].rearrange("q r e -> q (r e)")),
@@ -152,8 +154,6 @@ def tile_vc_interaction_sa_module_pa_t_kernel(tc, x, W_psi, b_psi, x_phi, x_thet
             )
 
         def exponentials(n, t):
-            if not live(n):
-                return
             if t == 0:
                 exp_sum[n] = work.tile([P, QUARTERS], F32, name="exp_sum")
                 expo[n] = work.tile([P, QUARTERS, TOKENS], F32, name="expo")
@@ -166,19 +166,16 @@ def tile_vc_interaction_sa_module_pa_t_kernel(tc, x, W_psi, b_psi, x_phi, x_thet
                 accum_out=exp_sum[n][:, t : t + 1],
             )
 
-        def fetch_out(n):
-            if not live(n):
-                return
-            out_sb[n] = work.tile([P, QUARTERS * FEATURES], F32, name="out_sb")
-            for b in range(QUARTERS // 2):
-                nc.scalar.copy(
-                    out=out_sb[n][:, 2 * b * FEATURES : 2 * (b + 1) * FEATURES],
-                    in_=out_bank[n, b][:].rearrange("p c a -> p (c a)"),
-                )
+        def fetch_out(n, b):
+            if b == 0:
+                out_sb[n] = work.tile([P, QUARTERS * FEATURES], F32, name="out_sb")
+            copy = nc.vector.tensor_copy if fetch_on_vector(n, b) else nc.scalar.copy
+            copy(
+                out=out_sb[n][:, 2 * b * FEATURES : 2 * (b + 1) * FEATURES],
+                in_=out_bank[n, b][:].rearrange("p c a -> p (c a)"),
+            )
 
         def maximum(n, t):
-            if not live(n):
-                return
             if t == 0:
                 neg_max[n] = work.tile([P, QUARTERS], F32, name="neg_max")
             nc.vector.tensor_reduce(
@@ -190,8 +187,6 @@ def tile_vc_interaction_sa_module_pa_t_kernel(tc, x, W_psi, b_psi, x_phi, x_thet
             )
 
         def quantise_x(n):
-            if not live(n):
-                return
             x_codes[n] = work.tile([P, QUARTERS * PASSES * P], U32, name="x_codes", align_bytes=64)
             x_scales[n] = work.tile([P, QUARTERS * PASSES * P], U8, name="x_scales", align_bytes=64)
             nc.vector.quantize_mx(
@@ -200,122 +195,167 @@ def tile_vc_interaction_sa_module_pa_t_kernel(tc, x, W_psi, b_psi, x_phi, x_thet
                 in_=x_grouped[n][:].rearrange("q t w -> q (t w)"),
             )
 
-        def add_bias(n):
-            if not live(n):
-                return
-            x3_grouped[n] = work.tile([P, FEATURES * PACK], BF16, name="x3_grouped", align_bytes=64)
-            for h in range(HALVES):
-                feats = slice(h * P, (h + 1) * P)
-                nc.vector.tensor_tensor(
-                    out=x3_grouped[n][:].rearrange("p (a t) -> p a t", t=QUARTERS)[:, feats, :],
-                    in0=x3_bank[n, h][:].rearrange("p t a -> p a t"),
-                    in1=bias[:, feats].unsqueeze(2).to_broadcast([P, P, QUARTERS]),
-                    op=mybir.AluOpType.add,
-                )
+        def add_bias(n, h):
+            if h == 0:
+                x3_grouped[n] = work.tile([P, FEATURES * PACK], BF16, name="x3_grouped", align_bytes=64)
+            feats = slice(h * P, (h + 1) * P)
+            nc.vector.tensor_tensor(
+                out=x3_grouped[n][:].rearrange("p (a t) -> p a t", t=QUARTERS)[:, feats, :],
+                in0=x3_bank[n, h][:].rearrange("p t a -> p a t"),
+                in1=bias[:, feats].unsqueeze(2).to_broadcast([P, P, QUARTERS]),
+                op=mybir.AluOpType.add,
+            )
 
         def quantise_x3(n):
-            if not live(n):
-                return
             x3_codes[n] = work.tile([P, FEATURES], U32, name="x3_codes", align_bytes=64)
             x3_scales[n] = work.tile([P, FEATURES], U8, name="x3_scales", align_bytes=64)
             nc.vector.quantize_mx(out=x3_codes[n][:].bitcast(FP8X4), scales=x3_scales[n][:], in_=x3_grouped[n][:])
 
         def reciprocal_of_sums(n):
-            if not live(n):
-                return
             inv_sum[n] = work.tile([P, QUARTERS], F32, name="inv_sum")
             nc.vector.reciprocal(out=inv_sum[n][:], in_=exp_sum[n][:])
-
-        def normalise_on_gpsimd(n):
-            if not live(n):
-                return
             cov_grouped[n] = work.tile([P, TOKENS * PACK], BF16, name="cov_grouped", align_bytes=64)
+
+        def normalise_on_gpsimd(n, first, last):
             nc.gpsimd.tensor_tensor(
-                out=cov_grouped[n][:, VECTOR_COLUMNS * PACK :].rearrange("p (i t) -> p i t", t=QUARTERS),
-                in0=expo[n][:, :, VECTOR_COLUMNS:].rearrange("p t i -> p i t"),
-                in1=inv_sum[n][:].unsqueeze(1).to_broadcast([P, GPSIMD_COLUMNS, QUARTERS]),
+                out=cov_grouped[n][:, first * PACK : last * PACK].rearrange("p (i t) -> p i t", t=QUARTERS),
+                in0=expo[n][:, :, first:last].rearrange("p t i -> p i t"),
+                in1=inv_sum[n][:].unsqueeze(1).to_broadcast([P, last - first, QUARTERS]),
                 op=mybir.AluOpType.mult,
             )
 
-        def normalise_on_vector(n):
-            if not live(n):
-                return
+        def normalise_on_vector(n, first, last):
             nc.vector.tensor_tensor(
-                out=cov_grouped[n][:, : VECTOR_COLUMNS * PACK].rearrange("p (c i t) -> p c t i", i=RUN, t=QUARTERS),
-                in0=expo[n][:, :, :VECTOR_COLUMNS].rearrange("p t (c i) -> p c t i", i=RUN),
-                in1=inv_sum[n][:].unsqueeze(1).unsqueeze(3).to_broadcast([P, VECTOR_COLUMNS // RUN, QUARTERS, RUN]),
+                out=cov_grouped[n][:, first * PACK : last * PACK].rearrange("p (c i t) -> p c t i", i=RUN, t=QUARTERS),
+                in0=expo[n][:, :, first:last].rearrange("p t (c i) -> p c t i", i=RUN),
+                in1=inv_sum[n][:].unsqueeze(1).unsqueeze(3).to_broadcast([P, (last - first) // RUN, QUARTERS, RUN]),
                 op=mybir.AluOpType.mult,
             )
 
-        def quantise_cov(n):
-            if not live(n):
-                return
-            cov_codes[n] = work.tile([P, TOKENS], U32, name="cov_codes", align_bytes=64)
-            cov_scales[n] = work.tile([P, TOKENS], U8, name="cov_scales", align_bytes=64)
-            nc.vector.quantize_mx(out=cov_codes[n][:].bitcast(FP8X4), scales=cov_scales[n][:], in_=cov_grouped[n][:])
+        def quantise_cov(n, first, last):
+            if first == 0:
+                cov_codes[n] = work.tile([P, TOKENS], U32, name="cov_codes", align_bytes=64)
+                cov_scales[n] = work.tile([P, TOKENS], U8, name="cov_scales", align_bytes=64)
+            nc.vector.quantize_mx(
+                out=cov_codes[n][:, first:last].bitcast(FP8X4),
+                scales=cov_scales[n][:, first:last],
+                in_=cov_grouped[n][:, first * PACK : last * PACK],
+            )
 
         ident = consts.tile([P, P], F32, name="ident")
         make_identity(nc, ident[:])
         w_sb = consts.tile([P, HALVES * CHANNELS], BF16, name="w_sb")
-        nc.sync.dma_start(
-            out=w_sb[:].rearrange("p (h c) -> p h c", h=HALVES),
-            in_=W_psi.rearrange("(h p) c -> p h c", p=P),
-        )
-        load_sample(0)
-        load_sample(1)
         bias = consts.tile([P, FEATURES], BF16, name="bias")
         nc.scalar.dma_start(out=bias[:], in_=b_psi.partition_broadcast(P))
-
         w_grouped = consts.tile([P, PASSES * FEATURES * PACK], BF16, name="w_grouped", align_bytes=64)
-        for h in range(HALVES):
-            w_bank = psum_tr.tile([P, WORD_BLOCKS, P], F32, name="w_bank", tag="tr")
-            for v in range(WORD_BLOCKS):
-                col = (h * WORD_BLOCKS + v) * P
-                nc.tensor.transpose(w_bank[:, v, :], words(w_sb[:])[:, col : col + P], ident[:])
-            nc.vector.tensor_copy(
-                out=words(w_grouped[:]).rearrange("q (g a u) -> q g a u", g=PASSES, u=PAIR)[:, :, h * P : (h + 1) * P, :],
-                in_=grouped_read(w_bank),
-            )
         w_codes = consts.tile([P, PASSES * FEATURES], U32, name="w_codes", align_bytes=64)
         w_scales = consts.tile([P, PASSES * FEATURES], U8, name="w_scales", align_bytes=64)
-        nc.vector.quantize_mx(out=w_codes[:].bitcast(FP8X4), scales=w_scales[:], in_=w_grouped[:])
+        w_bank = {}
 
-        for step in range(-QUARTERS, QUARTERS * SAMPLES + 10):
-            n, t = divmod(step, QUARTERS)
+        def load_w():
+            nc.sync.dma_start(
+                out=w_sb[:].rearrange("p (h c) -> p h c", h=HALVES),
+                in_=W_psi.rearrange("(h p) c -> p h c", p=P),
+            )
 
-            if t == 1:
-                store_sample(n - 3)
-            if t == 2:
-                load_sample(n + 3)
+        def transpose_w(h):
+            w_bank[h] = psum_tr.tile([P, WORD_BLOCKS, P], F32, name="w_bank", tag="tr")
+            for v in range(WORD_BLOCKS):
+                col = (h * WORD_BLOCKS + v) * P
+                nc.tensor.transpose(w_bank[h][:, v, :], words(w_sb[:])[:, col : col + P], ident[:])
 
-            group_x(*divmod(step + 1, QUARTERS))
-            if t == 1:
-                keep_features(phi_t, "phi_t", n + 1)
-            if t == 3:
-                keep_features(theta_t, "theta_t", n + 1)
-            exponentials(*divmod(step - 2, QUARTERS))
-            if t == 0:
-                fetch_out(n - 3)
+        def group_w(h):
+            nc.vector.tensor_copy(
+                out=words(w_grouped[:]).rearrange("q (g a u) -> q g a u", g=PASSES, u=PAIR)[:, :, h * P : (h + 1) * P, :],
+                in_=grouped_read(w_bank[h]),
+            )
 
-            if t == 2:
-                reciprocal_of_sums(n - 1)
-                normalise_on_gpsimd(n - 1)
-            maximum(*divmod(step - 1, QUARTERS))
-            if t == 0:
-                quantise_x(n - 1)
-            if t == 1:
-                normalise_on_vector(n - 2)
-                quantise_x3(n - 2)
-                quantise_cov(n - 2)
-            if t == 2:
-                add_bias(n - 1)
+        def quantise_w():
+            nc.vector.quantize_mx(out=w_codes[:].bitcast(FP8X4), scales=w_scales[:], in_=w_grouped[:])
 
-            scores_and_x_transposes(n, t, *divmod(step + 2, QUARTERS))
-            if t == 0:
-                transpose_features(phi_sb, n + 1)
-            if t == 2:
-                transpose_features(theta_sb, n + 1)
-            if t == 1:
-                project(n - 1)
-            if t == 3:
-                attend(n - 2)
+
+        def weights_in(n, h):
+            if n == 0:
+                transpose_w(h)
+
+        def weights_out(n, h):
+            if n == 0:
+                group_w(h)
+            if n == 0 and h == HALVES - 1:
+                quantise_w()
+
+        def keep_phi(n):
+            keep_features(phi_t, "phi_t", n)
+
+        def keep_theta(n):
+            keep_features(theta_t, "theta_t", n)
+
+        def transpose_phi(n):
+            transpose_features(phi_sb, n)
+
+        def transpose_theta(n):
+            transpose_features(theta_sb, n)
+
+        def x_quarter(n, s):
+            transpose_x(n, s, 0)
+            transpose_x(n, s, 1)
+
+        def both_scores(n, t):
+            scores(n, t, 0)
+            scores(n, t, 1)
+
+        def normalise_gp(n):
+            if n < SAMPLES - 1:
+                normalise_on_gpsimd(n, TOKENS - GP, TOKENS)
+
+        def normalise_v(n):
+            if n < SAMPLES - 1:
+                normalise_on_vector(n, 0, TOKENS - GP)
+                return
+            for first in (0, TOKENS // 2):
+                normalise_on_vector(n, first, first + TOKENS // 2)
+                quantise_cov(n, first, first + TOKENS // 2)
+
+        def quantise_c(n):
+            if n < SAMPLES - 1:
+                quantise_cov(n, 0, TOKENS)
+
+        def store_half(n, b):
+            if n == SAMPLES - 1:
+                store(n, b)
+            elif b == 1:
+                store_all(n)
+
+        load_features(0)
+        load_x(0)
+        load_features(1)
+        load_w()
+        load_x(1)
+        done = {(load_features, 0, ()), (load_x, 0, ()), (load_features, 1, ()), (load_x, 1, ())}
+        timetable = [
+            (0, -2, load_features, ()),
+            (1, 3, store_half, (0,)),
+            (2, 3, store_half, (1,)),
+            (1, -2, load_x, ()),
+            (0, 1, exponentials, (2,)), (0, 0, group_x, (1,)), (0, 3, fetch_out, (0,)),
+            (0, 1, maximum, (3,)), (0, 1, quantise_x, ()),
+            (0, 0, both_scores, (0,)), (0, 3, attend, (1,)), (0, -1, transpose_phi, ()), (0, 0, x_quarter, (2,)),
+            (0, 0, weights_in, (0,)),
+            (1, 1, exponentials, (3,)), (1, 3, fetch_out, (1,)), (1, -1, keep_phi, ()),
+            (1, 0, maximum, (0,)), (1, 0, weights_out, (0,)), (1, 2, normalise_v, ()), (1, 2, quantise_x3, ()), (1, 2, quantise_c, ()),
+            (1, 1, reciprocal_of_sums, ()), (1, 1, normalise_gp, ()),
+            (1, 0, both_scores, (1,)), (1, 0, x_quarter, (3,)), (1, 1, project, ()),
+            (1, 0, weights_in, (1,)),
+            (2, 0, exponentials, (0,)), (2, 0, group_x, (2,)), (2, 0, group_x, (3,)),
+            (2, 0, maximum, (1,)), (2, 0, weights_out, (1,)), (2, 1, add_bias, (0,)),
+            (2, 0, both_scores, (2,)), (2, -1, transpose_theta, ()), (2, -1, x_quarter, (0,)),
+            (3, 0, exponentials, (1,)), (3, -1, keep_theta, ()), (3, -1, group_x, (0,)),
+            (3, 0, maximum, (2,)), (3, 1, add_bias, (1,)),
+            (3, 0, both_scores, (3,)), (3, -1, x_quarter, (1,)), (3, 2, attend, (0,)),
+        ]
+        for step in range(-4, QUARTERS * SAMPLES + 14):
+            period, phase = divmod(step, QUARTERS)
+            for at, lag, op, args in timetable:
+                n = period - lag
+                if at == phase and 0 <= n < SAMPLES and (op, n, args) not in done:
+                    op(n, *args)

@@ -218,9 +218,9 @@ def tile_vc_interaction_sa_module_pa_t_kernel(tc, x, W_psi, b_psi, x_phi, x_thet
 
         def normalise_on_gpsimd(n, first, last):
             nc.gpsimd.tensor_tensor(
-                out=cov_grouped[n][:, first * PACK : last * PACK].rearrange("p (i t) -> p i t", t=QUARTERS),
-                in0=expo[n][:, :, first:last].rearrange("p t i -> p i t"),
-                in1=inv_sum[n][:].unsqueeze(1).to_broadcast([P, last - first, QUARTERS]),
+                out=cov_grouped[n][:, first * PACK : last * PACK].rearrange("p (c i t) -> p c t i", i=RUN, t=QUARTERS),
+                in0=expo[n][:, :, first:last].rearrange("p t (c i) -> p c t i", i=RUN),
+                in1=inv_sum[n][:].unsqueeze(1).unsqueeze(3).to_broadcast([P, (last - first) // RUN, QUARTERS, RUN]),
                 op=mybir.AluOpType.mult,
             )
 

@@ -18,7 +18,7 @@ PASSES = CHANNELS // (P * PACK)
 HALVES = FEATURES // P
 WORD_BLOCKS = CHANNELS // (P * PAIR)
 RUN = 4
-GP = 256
+GP = 288
 TR_BANKS, SC_BANKS, MX_BANKS = 3, 3, 2
 X_PIECES = {0: 4}
 
@@ -124,11 +124,14 @@ def tile_vc_interaction_sa_module_pa_t_kernel(tc, x, W_psi, b_psi, x_phi, x_thet
                         )
 
         def attend(n, b):
-            out_bank[n, b] = psum_mx.tile([P, 2, FEATURES], F32, name="out_bank", tag="mx")
+            apart = n == SAMPLES - 1 and b == 1
             for c in range(2):
+                if c == 0 or apart:
+                    bank = psum_mx.tile([P, 2, FEATURES], F32, name="out_bank", tag="mx")
+                    out_bank[n, b] = out_bank.get((n, b), ()) + (bank,)
                 cols = slice((2 * b + c) * P, (2 * b + c + 1) * P)
                 nc.tensor.matmul_mx(
-                    out=out_bank[n, b][:, c, :],
+                    out=bank[:, c, :],
                     lhsT=cov_codes[n][:, cols].bitcast(FP8X4),
                     lhsT_scale=cov_scales[n][:, cols],
                     rhs=x3_codes[n][:].bitcast(FP8X4),
@@ -146,9 +149,9 @@ def tile_vc_interaction_sa_module_pa_t_kernel(tc, x, W_psi, b_psi, x_phi, x_thet
                 in_=grouped_read(x_bank[n, t]),
             )
 
-        def keep_features(target, name, n):
+        def keep_features(target, name, n, copy):
             target[n] = work.tile([P, TOKENS, PAIR], BF16, name=name)
-            nc.scalar.copy(
+            copy(
                 out=words(target[n][:].rearrange("q r e -> q (r e)")),
                 in_=feat_bank[n][:].rearrange("q t r -> q (t r)"),
             )
@@ -169,11 +172,19 @@ def tile_vc_interaction_sa_module_pa_t_kernel(tc, x, W_psi, b_psi, x_phi, x_thet
         def fetch_out(n, b):
             if b == 0:
                 out_sb[n] = work.tile([P, QUARTERS * FEATURES], F32, name="out_sb")
-            copy = nc.vector.tensor_copy if fetch_on_vector(n, b) else nc.scalar.copy
-            copy(
-                out=out_sb[n][:, 2 * b * FEATURES : 2 * (b + 1) * FEATURES],
-                in_=out_bank[n, b][:].rearrange("p c a -> p (c a)"),
-            )
+            if len(out_bank[n, b]) == 1:
+                nc.scalar.copy(
+                    out=out_sb[n][:, 2 * b * FEATURES : 2 * (b + 1) * FEATURES],
+                    in_=out_bank[n, b][0][:].rearrange("p c a -> p (c a)"),
+                )
+                return
+            for c, copy in enumerate((nc.scalar.copy, nc.vector.tensor_copy)):
+                first = (2 * b + c) * FEATURES
+                copy(out=out_sb[n][:, first : first + FEATURES], in_=out_bank[n, b][c][:, c, :])
+                nc.sync.dma_start(
+                    out=by_quarters(out[n])[:, first : first + FEATURES],
+                    in_=out_sb[n][:, first : first + FEATURES],
+                )
 
         def maximum(n, t):
             if t == 0:
@@ -285,10 +296,10 @@ def tile_vc_interaction_sa_module_pa_t_kernel(tc, x, W_psi, b_psi, x_phi, x_thet
                 quantise_w()
 
         def keep_phi(n):
-            keep_features(phi_t, "phi_t", n)
+            keep_features(phi_t, "phi_t", n, nc.scalar.copy)
 
         def keep_theta(n):
-            keep_features(theta_t, "theta_t", n)
+            keep_features(theta_t, "theta_t", n, nc.scalar.copy)
 
         def transpose_phi(n):
             transpose_features(phi_sb, n)
@@ -308,22 +319,40 @@ def tile_vc_interaction_sa_module_pa_t_kernel(tc, x, W_psi, b_psi, x_phi, x_thet
             if n < SAMPLES - 1:
                 normalise_on_gpsimd(n, TOKENS - GP, TOKENS)
 
+        def normalise_on_scalar(n, first, last):
+            by_quarter = cov_grouped[n][:, first * PACK : last * PACK].rearrange("p (i t) -> p t i", t=QUARTERS)
+            for t in range(QUARTERS):
+                nc.scalar.activation(
+                    out=by_quarter[:, t, :],
+                    in_=expo[n][:, t, first:last],
+                    func=mybir.ActivationFunctionType.Copy,
+                    scale=inv_sum[n][:, t : t + 1],
+                )
+
         def normalise_v(n):
             if n < SAMPLES - 1:
                 normalise_on_vector(n, 0, TOKENS - GP)
                 return
-            for first in (0, TOKENS // 2):
-                normalise_on_vector(n, first, first + TOKENS // 2)
-                quantise_cov(n, first, first + TOKENS // 2)
+            quantise_x3(n)
+            half = TOKENS // 2
+            normalise_on_scalar(n, half + P, TOKENS)
+            normalise_on_vector(n, 0, half)
+            quantise_cov(n, 0, half)
+            normalise_on_vector(n, half, half + P)
+            quantise_cov(n, half, TOKENS)
+
+        def quantise_3(n):
+            if n < SAMPLES - 1:
+                quantise_x3(n)
 
         def quantise_c(n):
             if n < SAMPLES - 1:
                 quantise_cov(n, 0, TOKENS)
 
         def store_half(n, b):
-            if n == SAMPLES - 1:
+            if n == SAMPLES - 1 and b == 0:
                 store(n, b)
-            elif b == 1:
+            elif n < SAMPLES - 1 and b == 1:
                 store_all(n)
 
         load_features(0)
@@ -342,7 +371,7 @@ def tile_vc_interaction_sa_module_pa_t_kernel(tc, x, W_psi, b_psi, x_phi, x_thet
             (0, 0, both_scores, (0,)), (0, 3, attend, (1,)), (0, -1, transpose_phi, ()), (0, 0, x_quarter, (2,)),
             (0, 0, weights_in, (0,)),
             (1, 1, exponentials, (3,)), (1, 3, fetch_out, (1,)), (1, -1, keep_phi, ()),
-            (1, 0, maximum, (0,)), (1, 0, weights_out, (0,)), (1, 2, normalise_v, ()), (1, 2, quantise_x3, ()), (1, 2, quantise_c, ()),
+            (1, 0, maximum, (0,)), (1, 0, weights_out, (0,)), (1, 2, normalise_v, ()), (1, 2, quantise_3, ()), (1, 2, quantise_c, ()),
             (1, 1, reciprocal_of_sums, ()), (1, 1, normalise_gp, ()),
             (1, 0, both_scores, (1,)), (1, 0, x_quarter, (3,)), (1, 1, project, ()),
             (1, 0, weights_in, (1,)),

@@ -292,8 +292,16 @@ def tile_vc_interaction_sa_module_pa_t_kernel(tc, x, W_psi, b_psi, x_phi, x_thet
         def weights_out(n, h):
             if n == 0:
                 group_w(h)
-            if n == 0 and h == HALVES - 1:
+
+        def weights_done(n):
+            if n == 0:
                 quantise_w()
+
+        def but_second(op):
+            return lambda n, *args: op(n, *args) if n != 1 else None
+
+        def second(op):
+            return lambda n, *args: op(n, *args) if n == 1 else None
 
         def keep_phi(n):
             keep_features(phi_t, "phi_t", n, nc.scalar.copy)
@@ -329,9 +337,13 @@ def tile_vc_interaction_sa_module_pa_t_kernel(tc, x, W_psi, b_psi, x_phi, x_thet
                     scale=inv_sum[n][:, t : t + 1],
                 )
 
+        def normalise_s(n):
+            if n == SAMPLES - 2:
+                normalise_on_scalar(n, P, TOKENS - GP)
+
         def normalise_v(n):
             if n < SAMPLES - 1:
-                normalise_on_vector(n, 0, TOKENS - GP)
+                normalise_on_vector(n, 0, P if n == SAMPLES - 2 else TOKENS - GP)
                 return
             quantise_x3(n)
             half = TOKENS // 2
@@ -358,29 +370,27 @@ def tile_vc_interaction_sa_module_pa_t_kernel(tc, x, W_psi, b_psi, x_phi, x_thet
         load_features(0)
         load_x(0)
         load_features(1)
-        load_w()
         load_x(1)
+        load_w()
         done = {(load_features, 0, ()), (load_x, 0, ()), (load_features, 1, ()), (load_x, 1, ())}
         timetable = [
             (0, -2, load_features, ()),
             (1, 3, store_half, (0,)),
             (2, 3, store_half, (1,)),
             (1, -2, load_x, ()),
-            (0, 1, exponentials, (2,)), (0, 0, group_x, (1,)), (0, 3, fetch_out, (0,)),
-            (0, 1, maximum, (3,)), (0, 1, quantise_x, ()),
-            (0, 0, both_scores, (0,)), (0, 3, attend, (1,)), (0, -1, transpose_phi, ()), (0, 0, x_quarter, (2,)),
-            (0, 0, weights_in, (0,)),
-            (1, 1, exponentials, (3,)), (1, 3, fetch_out, (1,)), (1, -1, keep_phi, ()),
-            (1, 0, maximum, (0,)), (1, 0, weights_out, (0,)), (1, 2, normalise_v, ()), (1, 2, quantise_3, ()), (1, 2, quantise_c, ()),
+            (0, 0, second(group_x), (0,)), (0, 1, exponentials, (2,)), (0, 0, group_x, (1,)), (0, 3, fetch_out, (0,)),
+            (0, 1, maximum, (3,)), (0, 1, quantise_x, ()), (0, 1, weights_out, (0,)), (0, 1, weights_out, (1,)),
+            (0, 0, both_scores, (0,)), (0, 3, attend, (1,)), (0, -1, but_second(transpose_phi), ()), (0, 0, x_quarter, (2,)),
+            (1, 1, exponentials, (3,)), (1, 3, fetch_out, (1,)), (1, -1, but_second(keep_phi), ()),
+            (1, 1, weights_done, ()), (1, 0, maximum, (0,)), (1, 2, normalise_v, ()), (1, 2, quantise_3, ()), (1, 2, quantise_c, ()),
             (1, 1, reciprocal_of_sums, ()), (1, 1, normalise_gp, ()),
-            (1, 0, both_scores, (1,)), (1, 0, x_quarter, (3,)), (1, 1, project, ()),
-            (1, 0, weights_in, (1,)),
-            (2, 0, exponentials, (0,)), (2, 0, group_x, (2,)), (2, 0, group_x, (3,)),
-            (2, 0, maximum, (1,)), (2, 0, weights_out, (1,)), (2, 1, add_bias, (0,)),
-            (2, 0, both_scores, (2,)), (2, -1, transpose_theta, ()), (2, -1, x_quarter, (0,)),
-            (3, 0, exponentials, (1,)), (3, -1, keep_theta, ()), (3, -1, group_x, (0,)),
+            (1, 0, both_scores, (1,)), (1, -1, second(transpose_phi), ()), (1, 0, x_quarter, (3,)), (1, 1, project, ()),
+            (2, 0, exponentials, (0,)), (2, -1, second(keep_phi), ()), (2, 0, group_x, (2,)), (2, 0, group_x, (3,)),
+            (2, 0, maximum, (1,)), (2, 1, add_bias, (0,)),
+            (2, 0, both_scores, (2,)), (2, -1, transpose_theta, ()), (2, -1, but_second(x_quarter), (0,)),
+            (3, 1, normalise_s, ()), (3, 0, exponentials, (1,)), (3, -1, keep_theta, ()), (3, -1, but_second(group_x), (0,)),
             (3, 0, maximum, (2,)), (3, 1, add_bias, (1,)),
-            (3, 0, both_scores, (3,)), (3, -1, x_quarter, (1,)), (3, 2, attend, (0,)),
+            (3, 0, both_scores, (3,)), (3, -1, second(x_quarter), (0,)), (3, -1, x_quarter, (1,)), (3, 2, attend, (0,)), (3, 0, weights_in, (0,)), (3, 0, weights_in, (1,)),
         ]
         for step in range(-4, QUARTERS * SAMPLES + 14):
             period, phase = divmod(step, QUARTERS)

from contextlib import ExitStack

import concourse.mybir as mybir
from concourse.masks import make_identity

F32 = mybir.dt.float32
BF16 = mybir.dt.bfloat16
U32 = mybir.dt.uint32
U8 = mybir.dt.uint8
FP8X4 = mybir.dt.float8_e4m3fn_x4

SAMPLES, TOKENS, CHANNELS, FEATURES = 16, 512, 1024, 256
P = 128
PACK = 4
PAIR = 2
QUARTERS = TOKENS // P
PASSES = CHANNELS // (P * PACK)
HALVES = FEATURES // P
WORD_BLOCKS = CHANNELS // (P * PAIR)
RUN = 4
GP = 288
TR_BANKS, SC_BANKS, MX_BANKS = 3, 3, 2
X_PIECES = {0: 4}


def group_on_vector(n, t):
    return False


def fetch_on_vector(n, b):
    return n == SAMPLES - 1 and b == 1


FLOPS = 2 * SAMPLES * TOKENS * (CHANNELS * FEATURES + 2 * TOKENS * FEATURES)


def tile_vc_interaction_sa_module_pa_t_kernel(tc, x, W_psi, b_psi, x_phi, x_theta, out):
    nc = tc.nc
    with ExitStack() as ctx:
        consts = ctx.enter_context(tc.tile_pool(name="consts", bufs=1))
        loads = ctx.enter_context(tc.tile_pool(name="loads", bufs=4))
        work = ctx.enter_context(tc.tile_pool(name="work", bufs=3))
        psum_tr = ctx.enter_context(tc.psum_pool(name="psum_tr", bufs=TR_BANKS))
        psum_sc = ctx.enter_context(tc.psum_pool(name="psum_sc", bufs=SC_BANKS))
        psum_mx = ctx.enter_context(tc.psum_pool(name="psum_mx", bufs=MX_BANKS))
        ctx.enter_context(tc.manual_schedule())

        x_sb, phi_sb, theta_sb = {}, {}, {}
        x_bank, x_grouped, x_codes, x_scales = {}, {}, {}, {}
        feat_bank, phi_t, theta_t = {}, {}, {}
        sc_bank, neg_max, exp_sum, inv_sum, expo = {}, {}, {}, {}, {}
        cov_grouped, cov_codes, cov_scales = {}, {}, {}
        x3_bank, x3_grouped, x3_codes, x3_scales = {}, {}, {}, {}
        out_bank, out_sb = {}, {}

        def by_quarters(rows):
            return rows.rearrange("(p t) w -> p (t w)", t=QUARTERS)

        def words(tile_ap):
            return tile_ap.bitcast(F32)

        def grouped_read(bank):
            return bank[:].rearrange("q (g u) r -> q g r u", g=PASSES)

        def load_features(n):
            phi_sb[n] = loads.tile([P, QUARTERS * FEATURES], BF16, name="phi_sb")
            nc.sync.dma_start(out=phi_sb[n][:], in_=by_quarters(x_phi[n]))
            theta_sb[n] = loads.tile([P, QUARTERS * FEATURES], BF16, name="theta_sb")
            nc.sync.dma_start(out=theta_sb[n][:], in_=by_quarters(x_theta[n]))

        def load_x(n):
            pieces = X_PIECES.get(n, 1)
            wide = QUARTERS * CHANNELS // pieces
            x_sb[n] = loads.tile([P, QUARTERS * CHANNELS], BF16, name="x_sb")
            for c in range(pieces):
                cols = slice(c * wide, (c + 1) * wide)
                nc.sync.dma_start(out=x_sb[n][:, cols], in_=by_quarters(x[n])[:, cols])

        def store(n, b):
            cols = slice(2 * b * FEATURES, 2 * (b + 1) * FEATURES)
            nc.sync.dma_start(out=by_quarters(out[n])[:, cols], in_=out_sb[n][:, cols])

        def store_all(n):
            nc.sync.dma_start(out=by_quarters(out[n]), in_=out_sb[n][:])

        def scores(n, t, e):
            if e == 0:
                sc_bank[n, t] = psum_sc.tile([P, TOKENS], F32, name="sc_bank")
            nc.tensor.matmul(
                out=sc_bank[n, t][:],
                lhsT=theta_t[n][:, t * P : (t + 1) * P, e],
                rhs=phi_t[n][:, :, e],
                start=(e == 0),
                stop=(e == PAIR - 1),
            )

        def transpose_x(n, s, half):
            if half == 0:
                x_bank[n, s] = psum_tr.tile([P, WORD_BLOCKS, P], F32, name="x_bank", tag="tr")
            for v in range(half * WORD_BLOCKS // 2, (half + 1) * WORD_BLOCKS // 2):
                col = (s * WORD_BLOCKS + v) * P
                nc.tensor.transpose(x_bank[n, s][:, v, :], words(x_sb[n][:])[:, col : col + P], ident[:])

        def transpose_features(source, n):
            feat_bank[n] = psum_tr.tile([P, QUARTERS, P], F32, name="feat_bank", tag="tr")
            for t in range(QUARTERS):
                nc.tensor.transpose(feat_bank[n][:, t, :], words(source[n][:])[:, t * P : (t + 1) * P], ident[:])

        def project(n):
            for h in range(HALVES):
                x3_bank[n, h] = psum_mx.tile([P, QUARTERS, P], F32, name="x3_bank", tag="mx")
                for t in range(QUARTERS):
                    for g in range(PASSES):
                        rows = slice((t * PASSES + g) * P, (t * PASSES + g + 1) * P)
                        cols = slice(g * FEATURES + h * P, g * FEATURES + (h + 1) * P)
                        nc.tensor.matmul_mx(
                            out=x3_bank[n, h][:, t, :],
                            lhsT=x_codes[n][:, rows].bitcast(FP8X4),
                            lhsT_scale=x_scales[n][:, rows],
                            rhs=w_codes[:, cols].bitcast(FP8X4),
                            rhs_scale=w_scales[:, cols],
                            start=(g == 0),
                            stop=(g == PASSES - 1),
                        )

        def attend(n, b):
            apart = n == SAMPLES - 1 and b == 1
            for c in range(2):
                if c == 0 or apart:
                    bank = psum_mx.tile([P, 2, FEATURES], F32, name="out_bank", tag="mx")
                    out_bank[n, b] = out_bank.get((n, b), ()) + (bank,)
                cols = slice((2 * b + c) * P, (2 * b + c + 1) * P)
                nc.tensor.matmul_mx(
                    out=bank[:, c, :],
                    lhsT=cov_codes[n][:, cols].bitcast(FP8X4),
                    lhsT_scale=cov_scales[n][:, cols],
                    rhs=x3_codes[n][:].bitcast(FP8X4),
                    rhs_scale=x3_scales[n][:],
                    start=True,
                    stop=True,
                )

        def group_x(n, t):
            if t == 0:
                x_grouped[n] = work.tile([P, QUARTERS, PASSES * P * PACK], BF16, name="x_grouped", align_bytes=64)
            copy = nc.vector.tensor_copy if group_on_vector(n, t) else nc.scalar.copy
            copy(
                out=words(x_grouped[n][:, t, :]).rearrange("q (g r u) -> q g r u", g=PASSES, u=PAIR),
                in_=grouped_read(x_bank[n, t]),
            )

        def keep_features(target, name, n, copy):
            target[n] = work.tile([P, TOKENS, PAIR], BF16, name=name)
            copy(
                out=words(target[n][:].rearrange("q r e -> q (r e)")),
                in_=feat_bank[n][:].rearrange("q t r -> q (t r)"),
            )

        def exponentials(n, t):
            if t == 0:
                exp_sum[n] = work.tile([P, QUARTERS], F32, name="exp_sum")
                expo[n] = work.tile([P, QUARTERS, TOKENS], F32, name="expo")
            nc.scalar.activation(
                out=expo[n][:, t, :],
                in_=sc_bank[n, t][:],
                func=mybir.ActivationFunctionType.Exp,
                bias=neg_max[n][:, t : t + 1],
                scale=1.0,
                accum_out=exp_sum[n][:, t : t + 1],
            )

        def fetch_out(n, b):
            if b == 0:
                out_sb[n] = work.tile([P, QUARTERS * FEATURES], F32, name="out_sb")
            if len(out_bank[n, b]) == 1:
                nc.scalar.copy(
                    out=out_sb[n][:, 2 * b * FEATURES : 2 * (b + 1) * FEATURES],
                    in_=out_bank[n, b][0][:].rearrange("p c a -> p (c a)"),
                )
                return
            for c, copy in enumerate((nc.scalar.copy, nc.vector.tensor_copy)):
                first = (2 * b + c) * FEATURES
                copy(out=out_sb[n][:, first : first + FEATURES], in_=out_bank[n, b][c][:, c, :])
                nc.sync.dma_start(
                    out=by_quarters(out[n])[:, first : first + FEATURES],
                    in_=out_sb[n][:, first : first + FEATURES],
                )

        def maximum(n, t):
            if t == 0:
                neg_max[n] = work.tile([P, QUARTERS], F32, name="neg_max")
            nc.vector.tensor_reduce(
                out=neg_max[n][:, t : t + 1],
                in_=sc_bank[n, t][:],
                axis=mybir.AxisListType.X,
                op=mybir.AluOpType.max,
                negate=True,
            )

        def quantise_x(n):
            x_codes[n] = work.tile([P, QUARTERS * PASSES * P], U32, name="x_codes", align_bytes=64)
            x_scales[n] = work.tile([P, QUARTERS * PASSES * P], U8, name="x_scales", align_bytes=64)
            nc.vector.quantize_mx(
                out=x_codes[n][:].bitcast(FP8X4),
                scales=x_scales[n][:],
                in_=x_grouped[n][:].rearrange("q t w -> q (t w)"),
            )

        def add_bias(n, h):
            if h == 0:
                x3_grouped[n] = work.tile([P, FEATURES * PACK], BF16, name="x3_grouped", align_bytes=64)
            feats = slice(h * P, (h + 1) * P)
            nc.vector.tensor_tensor(
                out=x3_grouped[n][:].rearrange("p (a t) -> p a t", t=QUARTERS)[:, feats, :],
                in0=x3_bank[n, h][:].rearrange("p t a -> p a t"),
                in1=bias[:, feats].unsqueeze(2).to_broadcast([P, P, QUARTERS]),
                op=mybir.AluOpType.add,
            )

        def quantise_x3(n):
            x3_codes[n] = work.tile([P, FEATURES], U32, name="x3_codes", align_bytes=64)
            x3_scales[n] = work.tile([P, FEATURES], U8, name="x3_scales", align_bytes=64)
            nc.vector.quantize_mx(out=x3_codes[n][:].bitcast(FP8X4), scales=x3_scales[n][:], in_=x3_grouped[n][:])

        def reciprocal_of_sums(n):
            inv_sum[n] = work.tile([P, QUARTERS], F32, name="inv_sum")
            nc.vector.reciprocal(out=inv_sum[n][:], in_=exp_sum[n][:])
            cov_grouped[n] = work.tile([P, TOKENS * PACK], BF16, name="cov_grouped", align_bytes=64)

        def normalise_on_gpsimd(n, first, last):
            nc.gpsimd.tensor_tensor(
                out=cov_grouped[n][:, first * PACK : last * PACK].rearrange("p (c i t) -> p c t i", i=RUN, t=QUARTERS),
                in0=expo[n][:, :, first:last].rearrange("p t (c i) -> p c t i", i=RUN),
                in1=inv_sum[n][:].unsqueeze(1).unsqueeze(3).to_broadcast([P, (last - first) // RUN, QUARTERS, RUN]),
                op=mybir.AluOpType.mult,
            )

        def normalise_on_vector(n, first, last):
            nc.vector.tensor_tensor(
                out=cov_grouped[n][:, first * PACK : last * PACK].rearrange("p (c i t) -> p c t i", i=RUN, t=QUARTERS),
                in0=expo[n][:, :, first:last].rearrange("p t (c i) -> p c t i", i=RUN),
                in1=inv_sum[n][:].unsqueeze(1).unsqueeze(3).to_broadcast([P, (last - first) // RUN, QUARTERS, RUN]),
                op=mybir.AluOpType.mult,
            )

        def quantise_cov(n, first, last):
            if first == 0:
                cov_codes[n] = work.tile([P, TOKENS], U32, name="cov_codes", align_bytes=64)
                cov_scales[n] = work.tile([P, TOKENS], U8, name="cov_scales", align_bytes=64)
            nc.vector.quantize_mx(
                out=cov_codes[n][:, first:last].bitcast(FP8X4),
                scales=cov_scales[n][:, first:last],
                in_=cov_grouped[n][:, first * PACK : last * PACK],
            )

        ident = consts.tile([P, P], F32, name="ident")
        make_identity(nc, ident[:])
        w_sb = consts.tile([P, HALVES * CHANNELS], BF16, name="w_sb")
        bias = consts.tile([P, FEATURES], BF16, name="bias")
        nc.scalar.dma_start(out=bias[:], in_=b_psi.partition_broadcast(P))
        w_grouped = consts.tile([P, PASSES * FEATURES * PACK], BF16, name="w_grouped", align_bytes=64)
        w_codes = consts.tile([P, PASSES * FEATURES], U32, name="w_codes", align_bytes=64)
        w_scales = consts.tile([P, PASSES * FEATURES], U8, name="w_scales", align_bytes=64)
        w_bank = {}

        def load_w():
            nc.sync.dma_start(
                out=w_sb[:].rearrange("p (h c) -> p h c", h=HALVES),
                in_=W_psi.rearrange("(h p) c -> p h c", p=P),
            )

        def transpose_w(h):
            w_bank[h] = psum_tr.tile([P, WORD_BLOCKS, P], F32, name="w_bank", tag="tr")
            for v in range(WORD_BLOCKS):
                col = (h * WORD_BLOCKS + v) * P
                nc.tensor.transpose(w_bank[h][:, v, :], words(w_sb[:])[:, col : col + P], ident[:])

        def group_w(h):
            nc.vector.tensor_copy(
                out=words(w_grouped[:]).rearrange("q (g a u) -> q g a u", g=PASSES, u=PAIR)[:, :, h * P : (h + 1) * P, :],
                in_=grouped_read(w_bank[h]),
            )

        def quantise_w():
            nc.vector.quantize_mx(out=w_codes[:].bitcast(FP8X4), scales=w_scales[:], in_=w_grouped[:])


        def weights_in(n, h):
            if n == 0:
                transpose_w(h)

        def weights_out(n, h):
            if n == 0:
                group_w(h)

        def weights_done(n):
            if n == 0:
                quantise_w()

        def but_second(op):
            return lambda n, *args: op(n, *args) if n != 1 else None

        def second(op):
            return lambda n, *args: op(n, *args) if n == 1 else None

        def keep_phi(n):
            keep_features(phi_t, "phi_t", n, nc.scalar.copy)

        def keep_theta(n):
            keep_features(theta_t, "theta_t", n, nc.scalar.copy)

        def transpose_phi(n):
            transpose_features(phi_sb, n)

        def transpose_theta(n):
            transpose_features(theta_sb, n)

        def x_quarter(n, s):
            transpose_x(n, s, 0)
            transpose_x(n, s, 1)

        def both_scores(n, t):
            scores(n, t, 0)
            scores(n, t, 1)

        def normalise_gp(n):
            if n < SAMPLES - 1:
                normalise_on_gpsimd(n, TOKENS - GP, TOKENS)

        def normalise_on_scalar(n, first, last):
            by_quarter = cov_grouped[n][:, first * PACK : last * PACK].rearrange("p (i t) -> p t i", t=QUARTERS)
            for t in range(QUARTERS):
                nc.scalar.activation(
                    out=by_quarter[:, t, :],
                    in_=expo[n][:, t, first:last],
                    func=mybir.ActivationFunctionType.Copy,
                    scale=inv_sum[n][:, t : t + 1],
                )

        def normalise_s(n):
            if n == SAMPLES - 2:
                normalise_on_scalar(n, P, TOKENS - GP)

        def normalise_v(n):
            if n < SAMPLES - 1:
                normalise_on_vector(n, 0, P if n == SAMPLES - 2 else TOKENS - GP)
                return
            quantise_x3(n)
            half = TOKENS // 2
            normalise_on_scalar(n, half + P, TOKENS)
            normalise_on_vector(n, 0, half)
            quantise_cov(n, 0, half)
            normalise_on_vector(n, half, half + P)
            quantise_cov(n, half, TOKENS)

        def quantise_3(n):
            if n < SAMPLES - 1:
                quantise_x3(n)

        def quantise_c(n):
            if n < SAMPLES - 1:
                quantise_cov(n, 0, TOKENS)

        def store_half(n, b):
            if n == SAMPLES - 1 and b == 0:
                store(n, b)
            elif n < SAMPLES - 1 and b == 1:
                store_all(n)

        load_features(0)
        load_x(0)
        load_features(1)
        load_x(1)
        load_w()
        done = {(load_features, 0, ()), (load_x, 0, ()), (load_features, 1, ()), (load_x, 1, ())}
        timetable = [
            (0, -2, load_features, ()),
            (1, 3, store_half, (0,)),
            (2, 3, store_half, (1,)),
            (1, -2, load_x, ()),
            (0, 0, second(group_x), (0,)), (0, 1, exponentials, (2,)), (0, 0, group_x, (1,)), (0, 3, fetch_out, (0,)),
            (0, 1, maximum, (3,)), (0, 1, quantise_x, ()), (0, 1, weights_out, (0,)), (0, 1, weights_out, (1,)),
            (0, 0, both_scores, (0,)), (0, 3, attend, (1,)), (0, -1, but_second(transpose_phi), ()), (0, 0, x_quarter, (2,)),
            (1, 1, exponentials, (3,)), (1, 3, fetch_out, (1,)), (1, -1, but_second(keep_phi), ()),
            (1, 1, weights_done, ()), (1, 0, maximum, (0,)), (1, 2, normalise_v, ()), (1, 2, quantise_3, ()), (1, 2, quantise_c, ()),
            (1, 1, reciprocal_of_sums, ()), (1, 1, normalise_gp, ()),
            (1, 0, both_scores, (1,)), (1, -1, second(transpose_phi), ()), (1, 0, x_quarter, (3,)), (1, 1, project, ()),
            (2, 0, exponentials, (0,)), (2, -1, second(keep_phi), ()), (2, 0, group_x, (2,)), (2, 0, group_x, (3,)),
            (2, 0, maximum, (1,)), (2, 1, add_bias, (0,)),
            (2, 0, both_scores, (2,)), (2, -1, transpose_theta, ()), (2, -1, but_second(x_quarter), (0,)),
            (3, 1, normalise_s, ()), (3, 0, exponentials, (1,)), (3, -1, keep_theta, ()), (3, -1, but_second(group_x), (0,)),
            (3, 0, maximum, (2,)), (3, 1, add_bias, (1,)),
            (3, 0, both_scores, (3,)), (3, -1, second(x_quarter), (0,)), (3, -1, x_quarter, (1,)), (3, 2, attend, (0,)), (3, 0, weights_in, (0,)), (3, 0, weights_in, (1,)),
        ]
        for step in range(-4, QUARTERS * SAMPLES + 14):
            period, phase = divmod(step, QUARTERS)
            for at, lag, op, args in timetable:
                n = period - lag
                if at == phase and 0 <= n < SAMPLES and (op, n, args) not in done:
                    op(n, *args)
